import numpy as np
import ml_dtypes


def mxq(x, axis, fmt="e4m3"):
    dtype, down = {"e4m3": (ml_dtypes.float8_e4m3fn, 7), "e5m2": (ml_dtypes.float8_e5m2, 14)}[fmt]
    v = np.moveaxis(np.asarray(x, np.float32).astype(ml_dtypes.bfloat16).astype(np.float64), axis, -1)
    blocks = v.reshape(v.shape[:-1] + (-1, 32))
    amax = np.abs(blocks).max(-1, keepdims=True)
    byte = np.maximum(np.where(amax > 0, np.frexp(amax)[1] - 1 + 127, 0) - down, 1)
    scale = np.exp2(byte - 127.0)
    codes = (blocks / scale).astype(np.float32).astype(dtype).astype(np.float64)
    return np.moveaxis((codes * scale).reshape(v.shape), -1, axis)


WIDE = False


def mx_kscale(k):
    if not WIDE:
        return np.ones(k)
    levels = np.array([10, -10, 5, -5, 0])
    a = np.random.permutation(np.resize(levels, k // 512 * 4)).reshape(k // 512, 4)
    idx = np.arange(k)
    return np.exp2(a[idx // 512, idx % 128 // 32])


BF16 = ml_dtypes.bfloat16


def bf(x):
    return np.asarray(x, np.float32).astype(BF16)


def f64(x):
    return np.asarray(x).astype(np.float64)


E2M1 = np.array([0.0, 0.5, 1.0, 1.5, 2.0, 3.0, 4.0, 6.0, -0.0, -0.5, -1.0, -1.5, -2.0, -3.0, -4.0, -6.0])


def pack_weight(w, fmt):
    k, n = w.shape
    w = f64(bf(w)).reshape(k // 32, 32, n)
    amax = np.abs(w).max(1)
    if fmt == "e4m3":
        byte = np.frexp(amax)[1] - 1 + 127 - 7
    else:
        mant, ex = np.frexp(amax / 6.0)
        byte = np.where(mant > 0.5, ex, ex - 1) + 127
    byte = np.clip(np.where(amax > 0, byte, 1), 1, 254)
    scaled = (w * np.exp2(127.0 - byte)[:, None, :]).reshape(k, n).astype(np.float32)
    by_word = np.ascontiguousarray(scaled.reshape(k // 512, 128, 4, n).transpose(0, 1, 3, 2))
    if fmt == "e4m3":
        words = by_word.astype(ml_dtypes.float8_e4m3fn).view(np.uint8)
    else:
        c = by_word.astype(ml_dtypes.float4_e2m1fn).view(np.uint8) & 0xF
        words = c[..., 0::2] | (c[..., 1::2] << 4)
    return np.ascontiguousarray(words), np.ascontiguousarray(byte.astype(np.uint8).reshape(k // 512, 16, n))


def unpack_weight(words, scales, fmt):
    g, p, n, _ = words.shape
    if fmt == "e4m3":
        vals = np.ascontiguousarray(words).view(ml_dtypes.float8_e4m3fn).astype(np.float64)
    else:
        nib = np.empty((g, p, n, 4), np.uint8)
        nib[..., 0::2] = words & 0xF
        nib[..., 1::2] = words >> 4
        vals = E2M1[nib]
    vals = vals * np.repeat(np.exp2(scales.astype(np.float64) - 127.0), 8, axis=1)[..., None]
    return vals.transpose(0, 1, 3, 2).reshape(g * 512, n)


B, L, N, RS, D, H, A, F = 4, 4, 128, 16, 512, 8, 64, 2048
S = L * (N + RS)
EPS = 1e-05
FMT = "e4m3"


def rmsnorm(x, w):
    return x / np.sqrt(np.mean(x * x, -1, keepdims=True) + EPS) * w


def silu(v):
    return v / (1.0 + np.exp(-v))


def setup_inputs():
    s, t = mx_kscale(D), mx_kscale(D)
    o_attn = bf(np.random.standard_normal((B, S, D)) * 0.14 * s)
    xm = bf(np.random.standard_normal((B, S, D)))
    attn_o_w_words, attn_o_w_scales = pack_weight(np.random.standard_normal((D, D)) * 3.0 / np.sqrt(D) / s[:, None], FMT)
    ffn_norm_w = bf((1.0 + 0.1 * np.random.standard_normal(D)) * t)
    ffn_up_w_words, ffn_up_w_scales = pack_weight(np.random.standard_normal((D, 2 * F)) / np.sqrt(D) / t[:, None], FMT)
    return {'o_attn': o_attn,
            'xm': xm,
            'attn_o_w_words': attn_o_w_words,
            'attn_o_w_scales': attn_o_w_scales,
            'ffn_norm_w': ffn_norm_w,
            'ffn_up_w_words': ffn_up_w_words,
            'ffn_up_w_scales': ffn_up_w_scales}


def reference(o_attn, xm, attn_o_w_words, attn_o_w_scales, ffn_norm_w, ffn_up_w_words, ffn_up_w_scales):
    x2 = (mxq(f64(o_attn), 2, 'e4m3') @ unpack_weight(attn_o_w_words, attn_o_w_scales, FMT)) + f64(xm)
    xn2 = rmsnorm(x2, f64(ffn_norm_w))
    u1, u2 = np.split(mxq(xn2, 2, 'e4m3') @ unpack_weight(ffn_up_w_words, ffn_up_w_scales, FMT), 2, axis=-1)
    return x2, silu(u1) * u2

@@ -1,0 +1,251 @@
+import math
+from contextlib import ExitStack
+
+import concourse.mybir as mybir
+from concourse.masks import make_identity
+
+F32 = mybir.dt.float32
+BF16 = mybir.dt.bfloat16
+I32 = mybir.dt.int32
+U32 = mybir.dt.uint32
+U8 = mybir.dt.uint8
+FP8X4 = mybir.dt.float8_e4m3fn_x4
+ALU = mybir.AluOpType
+ACT = mybir.ActivationFunctionType
+
+P = 128
+PACK = 4
+D = 512
+F = 2048
+BANK = 512
+TOKENS = 4 * 576
+TILES = TOKENS // P
+PAIRS = TILES // 2
+LOAD_TILES = 6
+STORE_BANKS = 2
+EPS = 1e-5
+
+FLOPS = 2 * TOKENS * D * (D + 2 * F)
+
+
+def load_scale_rows(nc, plane, scales):
+    for quadrant in range(4):
+        nc.sync.dma_start(
+            out=plane[32 * quadrant : 32 * quadrant + 4, :].bitcast(I32),
+            in_=scales[0, 4 * quadrant : 4 * quadrant + 4, :].bitcast(I32),
+        )
+
+
+def tile_model_pb_kernel(
+    tc,
+    o_attn,
+    xm,
+    attn_o_w_words,
+    attn_o_w_scales,
+    ffn_norm_w,
+    ffn_up_w_words,
+    ffn_up_w_scales,
+    out_0,
+    out_1,
+):
+    nc = tc.nc
+    o_dram = o_attn.flatten_outer_dims().rearrange("(p n) d -> p n d", n=TILES)
+    xm_dram = xm.flatten_outer_dims().rearrange("(p n) d -> p n d", n=TILES)
+    x2_dram = out_0.flatten_outer_dims().rearrange("(p n) d -> p n d", n=TILES)
+    h_dram = out_1.flatten_outer_dims().rearrange("(p n) f -> p n f", n=TILES)
+
+    with ExitStack() as pools:
+        keep = pools.enter_context(tc.tile_pool(name="keep", bufs=1))
+        work = pools.enter_context(tc.tile_pool(name="work", bufs=3))
+        gates = pools.enter_context(tc.tile_pool(name="gates", bufs=4))
+        results = pools.enter_context(tc.tile_pool(name="results", bufs=6))
+        banks = pools.enter_context(tc.psum_pool(name="banks", bufs=6))
+        flips = pools.enter_context(tc.psum_pool(name="flips", bufs=2))
+
+        o_all = keep.tile([P, TILES, D], BF16)
+        xm_all = keep.tile([P, TILES, D], BF16)
+        x2_all = keep.tile([P, TILES, D], F32)
+        xn2_all = keep.tile([P, TILES, D], BF16)
+        wo_codes = keep.tile([P, D], U32, align_bytes=64)
+        wo_plane = keep.tile([P, D], U8, align_bytes=64)
+        up_codes = keep.tile([P, 2 * F], U32, align_bytes=64)
+        up_plane = keep.tile([P, 2 * F], U8, align_bytes=64)
+        o_codes = keep.tile([P, TILES, P], U32, align_bytes=64)
+        o_planes = keep.tile([P, TILES, P], U8, align_bytes=64)
+        xn_codes = keep.tile([P, TILES, P], U32, align_bytes=64)
+        xn_planes = keep.tile([P, TILES, P], U8, align_bytes=64)
+        mean_sq = keep.tile([P, TILES], F32)
+        mean_sq_eps = keep.tile([P, TILES], F32)
+        rstd = keep.tile([P, TILES], F32)
+
+        gain_rows = keep.tile([P, D], BF16)
+        nc.vector.memset(gain_rows[:], 0.0)
+        nc.vector.memset(wo_plane[:].bitcast(I32), 0)
+        nc.vector.memset(up_plane[:].bitcast(I32), 0)
+        ident_f32 = keep.tile([P, P], F32)
+        make_identity(nc, ident_f32[:])
+        ident_bf16 = keep.tile([P, P], BF16)
+        make_identity(nc, ident_bf16[:])
+        ones = keep.tile([P, P], BF16)
+        nc.gpsimd.memset(ones[:], 1.0)
+        minus_half = keep.tile([P, 2], F32)
+        nc.gpsimd.memset(minus_half[:], -0.5)
+        warm_in = keep.tile([P, 1], F32)
+        warm_out = keep.tile([P, 1], F32)
+        nc.vector.memset(warm_in[:], 0.0)
+        nc.scalar.activation(out=warm_out[:], in_=warm_in[:], func=ACT.Silu)
+
+        def load_tokens(sbuf, dram, first):
+            tiles = slice(first, first + LOAD_TILES)
+            nc.sync.dma_start(out=sbuf[:, tiles, :], in_=dram[:, tiles, :])
+
+        load_tokens(o_all, o_dram, 0)
+        nc.sync.dma_start(out=gain_rows[0:1, :], in_=ffn_norm_w.rearrange("(o d) -> o d", o=1))
+        load_scale_rows(nc, wo_plane, attn_o_w_scales)
+        nc.sync.dma_start(
+            out=wo_codes[:].bitcast(I32),
+            in_=attn_o_w_words[0].rearrange("p n t -> p (n t)").bitcast(I32),
+        )
+        load_scale_rows(nc, up_plane, ffn_up_w_scales)
+        load_tokens(xm_all, xm_dram, 0)
+        for first in range(LOAD_TILES, TILES, LOAD_TILES):
+            load_tokens(o_all, o_dram, first)
+            load_tokens(xm_all, xm_dram, first)
+        up_words_dram = ffn_up_w_words[0].rearrange("p n t -> p (n t)").bitcast(I32)
+        for half in range(2):
+            columns = slice(half * F, (half + 1) * F)
+            nc.sync.dma_start(out=up_codes[:, columns].bitcast(I32), in_=up_words_dram[:, columns])
+
+        gain_bank = banks.tile([P, D], F32, tag="bank")
+        nc.tensor.matmul(out=gain_bank[:], lhsT=ones[:], rhs=gain_rows[:], start=True, stop=True)
+        gain = keep.tile([P, D], F32)
+        nc.scalar.copy(out=gain[:], in_=gain_bank[:])
+
+        def quantise_pair(grouped, codes, planes, m):
+            pair = slice(2 * m, 2 * m + 2)
+            nc.vector.quantize_mx(
+                out=codes[:, pair, :].rearrange("p a r -> p (a r)").bitcast(FP8X4),
+                scales=planes[:, pair, :].rearrange("p a r -> p (a r)"),
+                in_=grouped[:].rearrange("p a r t -> p (a r t)"),
+            )
+
+        def flip_attention(m):
+            o_words = o_all[:].bitcast(F32)
+            flipped = flips.tile([P, 2, 2, P], F32, tag="flip")
+            for a in range(2):
+                for u in range(2):
+                    nc.tensor.transpose(
+                        flipped[:, a, u, :], o_words[:, 2 * m + a, u : D // 2 : 2], ident_f32[:]
+                    )
+            grouped = work.tile([P, 2, P, PACK], BF16, tag="grouped", align_bytes=64)
+            nc.scalar.copy(
+                out=grouped[:].bitcast(F32), in_=flipped[:].rearrange("p a u r -> p a r u")
+            )
+            quantise_pair(grouped, o_codes, o_planes, m)
+
+        def project_and_norm(m):
+            pair = slice(2 * m, 2 * m + 2)
+            for n in range(2 * m, 2 * m + 2):
+                attn_bank = banks.tile([P, D], F32, tag="bank")
+                nc.tensor.matmul_mx(
+                    out=attn_bank[:],
+                    lhsT=o_codes[:, n, :].bitcast(FP8X4),
+                    lhsT_scale=o_planes[:, n, :],
+                    rhs=wo_codes[:].bitcast(FP8X4),
+                    rhs_scale=wo_plane[:],
+                    start=True,
+                    stop=True,
+                )
+                nc.vector.tensor_tensor(
+                    out=x2_all[:, n, :], in0=attn_bank[:], in1=xm_all[:, n, :], op=ALU.add
+                )
+                squares = work.tile([P, D], BF16, tag="squares")
+                nc.scalar.activation(
+                    out=squares[:],
+                    in_=x2_all[:, n, :],
+                    func=ACT.Square,
+                    scale=1.0 / math.sqrt(D),
+                    accum_out=mean_sq[:, n : n + 1],
+                )
+            nc.sync.dma_start(out=x2_dram[:, pair, :], in_=x2_all[:, pair, :])
+            nc.gpsimd.tensor_scalar(
+                out=mean_sq_eps[:, pair],
+                in0=mean_sq[:, pair],
+                scalar1=1.0,
+                scalar2=EPS,
+                op0=ALU.mult,
+                op1=ALU.add,
+            )
+            nc.gpsimd.tensor_tensor(
+                out=rstd[:, pair], in0=mean_sq_eps[:, pair], in1=minus_half[:], op=ALU.pow
+            )
+            scaled = work.tile([P, 2, D], F32, tag="scaled")
+            for a in range(2):
+                n = 2 * m + a
+                nc.gpsimd.tensor_scalar(
+                    out=scaled[:, a, :],
+                    in0=x2_all[:, n, :],
+                    scalar1=rstd[:, n : n + 1],
+                    scalar2=0.0,
+                    op0=ALU.mult,
+                    op1=ALU.add,
+                )
+            nc.gpsimd.tensor_tensor(
+                out=xn2_all[:, pair, :],
+                in0=scaled[:],
+                in1=gain[:].unsqueeze(1).to_broadcast([P, 2, D]),
+                op=ALU.mult,
+            )
+
+        def flip_normed(m):
+            flipped = flips.tile([P, 2, PACK, P], BF16, tag="flip")
+            for a in range(2):
+                for t in range(PACK):
+                    nc.tensor.transpose(
+                        flipped[:, a, t, :], xn2_all[:, 2 * m + a, t:D:PACK], ident_bf16[:]
+                    )
+            grouped = work.tile([P, 2, P, PACK], BF16, tag="grouped", align_bytes=64)
+            nc.scalar.copy(out=grouped[:], in_=flipped[:].rearrange("p a t r -> p a r t"))
+            return grouped
+
+        def gated_up(n):
+            for first in range(0, F // BANK, STORE_BANKS):
+                h_part = results.tile([P, STORE_BANKS, BANK], F32)
+                for b in range(STORE_BANKS):
+                    column = (first + b) * BANK
+                    halves = []
+                    for start in (column, F + column):
+                        u_bank = banks.tile([P, BANK], F32, tag="bank")
+                        nc.tensor.matmul_mx(
+                            out=u_bank[:],
+                            lhsT=xn_codes[:, n, :].bitcast(FP8X4),
+                            lhsT_scale=xn_planes[:, n, :],
+                            rhs=up_codes[:, start : start + BANK].bitcast(FP8X4),
+                            rhs_scale=up_plane[:, start : start + BANK],
+                            start=True,
+                            stop=True,
+                        )
+                        halves.append(u_bank)
+                    gate = gates.tile([P, BANK], F32)
+                    nc.scalar.activation(out=gate[:], in_=halves[0][:], func=ACT.Silu)
+                    nc.vector.tensor_tensor(
+                        out=h_part[:, b, :], in0=halves[1][:], in1=gate[:], op=ALU.mult
+                    )
+                nc.sync.dma_start(
+                    out=h_dram[:, n, first * BANK : (first + STORE_BANKS) * BANK],
+                    in_=h_part[:].rearrange("p b c -> p (b c)"),
+                )
+
+        flip_attention(0)
+        for m in range(PAIRS):
+            if m + 1 < PAIRS:
+                flip_attention(m + 1)
+            project_and_norm(m)
+        quantise_pair(flip_normed(0), xn_codes, xn_planes, 0)
+        for m in range(PAIRS):
+            gated_up(2 * m)
+            if m + 1 < PAIRS:
+                grouped_next = flip_normed(m + 1)
+            gated_up(2 * m + 1)
+            if m + 1 < PAIRS:
+                quantise_pair(grouped_next, xn_codes, xn_planes, m + 1)

@@ -179,23 +179,15 @@ def tile_model_pb_kernel(
             nc.gpsimd.tensor_tensor(
                 out=rstd[:, pair], in0=mean_sq_eps[:, pair], in1=minus_half[:], op=ALU.pow
             )
-            scaled = work.tile([P, 2, D], F32, tag="scaled")
-            for a in range(2):
-                n = 2 * m + a
-                nc.gpsimd.tensor_scalar(
-                    out=scaled[:, a, :],
+            for n in range(2 * m, 2 * m + 2):
+                nc.vector.scalar_tensor_tensor(
+                    out=xn2_all[:, n, :],
                     in0=x2_all[:, n, :],
-                    scalar1=rstd[:, n : n + 1],
-                    scalar2=0.0,
+                    scalar=rstd[:, n : n + 1],
+                    in1=gain[:],
                     op0=ALU.mult,
-                    op1=ALU.add,
+                    op1=ALU.mult,
                 )
-            nc.gpsimd.tensor_tensor(
-                out=xn2_all[:, pair, :],
-                in0=scaled[:],
-                in1=gain[:].unsqueeze(1).to_broadcast([P, 2, D]),
-                op=ALU.mult,
-            )
 
         def flip_normed(m):
             flipped = flips.tile([P, 2, PACK, P], BF16, tag="flip")

@@ -121,15 +121,24 @@ def tile_model_pb_kernel(
         gain = keep.tile([P, D], F32)
         nc.scalar.copy(out=gain[:], in_=gain_bank[:])
 
-        def quantise_pair(grouped, codes, planes, m):
+        held = {}
+
+        def exists(m):
+            return 0 <= m < PAIRS
+
+        def quantise_pair(name, codes, planes, m):
+            if not exists(m):
+                return
             pair = slice(2 * m, 2 * m + 2)
             nc.vector.quantize_mx(
                 out=codes[:, pair, :].rearrange("p a r -> p (a r)").bitcast(FP8X4),
                 scales=planes[:, pair, :].rearrange("p a r -> p (a r)"),
-                in_=grouped[:].rearrange("p a r t -> p (a r t)"),
+                in_=held[(name, m)][:].rearrange("p a r t -> p (a r t)"),
             )
 
         def flip_attention(m):
+            if not exists(m):
+                return
             o_words = o_all[:].bitcast(F32)
             flipped = flips.tile([P, 2, 2, P], F32, tag="flip")
             for a in range(2):
@@ -141,10 +150,11 @@ def tile_model_pb_kernel(
             nc.scalar.copy(
                 out=grouped[:].bitcast(F32), in_=flipped[:].rearrange("p a u r -> p a r u")
             )
-            quantise_pair(grouped, o_codes, o_planes, m)
+            held[("o grouped", m)] = grouped
 
-        def project_and_norm(m):
-            pair = slice(2 * m, 2 * m + 2)
+        def project(m):
+            if not exists(m):
+                return
             for n in range(2 * m, 2 * m + 2):
                 attn_bank = banks.tile([P, D], F32, tag="bank")
                 nc.tensor.matmul_mx(
@@ -156,9 +166,26 @@ def tile_model_pb_kernel(
                     start=True,
                     stop=True,
                 )
+                held[("attn bank", n)] = attn_bank
+
+        def add_residual(m):
+            if not exists(m):
+                return
+            pair = slice(2 * m, 2 * m + 2)
+            for n in range(2 * m, 2 * m + 2):
                 nc.vector.tensor_tensor(
-                    out=x2_all[:, n, :], in0=attn_bank[:], in1=xm_all[:, n, :], op=ALU.add
+                    out=x2_all[:, n, :],
+                    in0=held[("attn bank", n)][:],
+                    in1=xm_all[:, n, :],
+                    op=ALU.add,
                 )
+            nc.sync.dma_start(out=x2_dram[:, pair, :], in_=x2_all[:, pair, :])
+
+        def norm(m):
+            if not exists(m):
+                return
+            pair = slice(2 * m, 2 * m + 2)
+            for n in range(2 * m, 2 * m + 2):
                 squares = work.tile([P, D], BF16, tag="squares")
                 nc.scalar.activation(
                     out=squares[:],
@@ -167,7 +194,6 @@ def tile_model_pb_kernel(
                     scale=1.0 / math.sqrt(D),
                     accum_out=mean_sq[:, n : n + 1],
                 )
-            nc.sync.dma_start(out=x2_dram[:, pair, :], in_=x2_all[:, pair, :])
             nc.gpsimd.tensor_scalar(
                 out=mean_sq_eps[:, pair],
                 in0=mean_sq[:, pair],
@@ -179,65 +205,87 @@ def tile_model_pb_kernel(
             nc.gpsimd.tensor_tensor(
                 out=rstd[:, pair], in0=mean_sq_eps[:, pair], in1=minus_half[:], op=ALU.pow
             )
-            for n in range(2 * m, 2 * m + 2):
-                nc.vector.scalar_tensor_tensor(
-                    out=xn2_all[:, n, :],
+            scaled = work.tile([P, 2, D], F32, tag="scaled")
+            for a in range(2):
+                n = 2 * m + a
+                nc.gpsimd.tensor_scalar(
+                    out=scaled[:, a, :],
                     in0=x2_all[:, n, :],
-                    scalar=rstd[:, n : n + 1],
-                    in1=gain[:],
+                    scalar1=rstd[:, n : n + 1],
+                    scalar2=0.0,
                     op0=ALU.mult,
-                    op1=ALU.mult,
+                    op1=ALU.add,
                 )
+            nc.gpsimd.tensor_tensor(
+                out=xn2_all[:, pair, :],
+                in0=scaled[:],
+                in1=gain[:].unsqueeze(1).to_broadcast([P, 2, D]),
+                op=ALU.mult,
+            )
 
         def flip_normed(m):
+            if not exists(m):
+                return
             flipped = flips.tile([P, 2, PACK, P], BF16, tag="flip")
             for a in range(2):
                 for t in range(PACK):
                     nc.tensor.transpose(
                         flipped[:, a, t, :], xn2_all[:, 2 * m + a, t:D:PACK], ident_bf16[:]
                     )
+            held[("xn flipped", m)] = flipped
+
+        def group_normed(m):
+            if not exists(m):
+                return
             grouped = work.tile([P, 2, P, PACK], BF16, tag="grouped", align_bytes=64)
-            nc.scalar.copy(out=grouped[:], in_=flipped[:].rearrange("p a t r -> p a r t"))
-            return grouped
+            nc.scalar.copy(
+                out=grouped[:], in_=held[("xn flipped", m)][:].rearrange("p a t r -> p a r t")
+            )
+            held[("xn grouped", m)] = grouped
 
-        def gated_up(n):
-            for first in range(0, F // BANK, STORE_BANKS):
-                h_part = results.tile([P, STORE_BANKS, BANK], F32)
-                for b in range(STORE_BANKS):
-                    column = (first + b) * BANK
-                    halves = []
-                    for start in (column, F + column):
-                        u_bank = banks.tile([P, BANK], F32, tag="bank")
-                        nc.tensor.matmul_mx(
-                            out=u_bank[:],
-                            lhsT=xn_codes[:, n, :].bitcast(FP8X4),
-                            lhsT_scale=xn_planes[:, n, :],
-                            rhs=up_codes[:, start : start + BANK].bitcast(FP8X4),
-                            rhs_scale=up_plane[:, start : start + BANK],
-                            start=True,
-                            stop=True,
-                        )
-                        halves.append(u_bank)
-                    gate = gates.tile([P, BANK], F32)
-                    nc.scalar.activation(out=gate[:], in_=halves[0][:], func=ACT.Silu)
-                    nc.vector.tensor_tensor(
-                        out=h_part[:, b, :], in0=halves[1][:], in1=gate[:], op=ALU.mult
+        def gated_up(m, quarter):
+            if not exists(m):
+                return
+            n = 2 * m + quarter // 2
+            part = quarter % 2
+            h_part = results.tile([P, STORE_BANKS, BANK], F32)
+            for b in range(STORE_BANKS):
+                column = (part * STORE_BANKS + b) * BANK
+                gate_bank = banks.tile([P, BANK], F32, tag="bank")
+                value_bank = banks.tile([P, BANK], F32, tag="bank")
+                for u_bank, first in ((gate_bank, column), (value_bank, F + column)):
+                    nc.tensor.matmul_mx(
+                        out=u_bank[:],
+                        lhsT=xn_codes[:, n, :].bitcast(FP8X4),
+                        lhsT_scale=xn_planes[:, n, :],
+                        rhs=up_codes[:, first : first + BANK].bitcast(FP8X4),
+                        rhs_scale=up_plane[:, first : first + BANK],
+                        start=True,
+                        stop=True,
                     )
-                nc.sync.dma_start(
-                    out=h_dram[:, n, first * BANK : (first + STORE_BANKS) * BANK],
-                    in_=h_part[:].rearrange("p b c -> p (b c)"),
+                gate = gates.tile([P, BANK], F32)
+                nc.scalar.activation(out=gate[:], in_=gate_bank[:], func=ACT.Silu)
+                nc.vector.tensor_tensor(
+                    out=h_part[:, b, :], in0=value_bank[:], in1=gate[:], op=ALU.mult
                 )
+            width = STORE_BANKS * BANK
+            nc.sync.dma_start(
+                out=h_dram[:, n, part * width : (part + 1) * width],
+                in_=h_part[:].rearrange("p b c -> p (b c)"),
+            )
 
-        flip_attention(0)
-        for m in range(PAIRS):
-            if m + 1 < PAIRS:
-                flip_attention(m + 1)
-            project_and_norm(m)
-        quantise_pair(flip_normed(0), xn_codes, xn_planes, 0)
-        for m in range(PAIRS):
-            gated_up(2 * m)
-            if m + 1 < PAIRS:
-                grouped_next = flip_normed(m + 1)
-            gated_up(2 * m + 1)
-            if m + 1 < PAIRS:
-                quantise_pair(grouped_next, xn_codes, xn_planes, m + 1)
+        with tc.manual_schedule():
+            for j in range(-1, 2 * PAIRS):
+                m = j - PAIRS
+                flip_attention(j + 1)
+                project(j)
+                gated_up(m, 0)
+                group_normed(m + 1)
+                gated_up(m, 1)
+                add_residual(j)
+                flip_normed(m + 2)
+                quantise_pair("xn grouped", xn_codes, xn_planes, m + 1)
+                gated_up(m, 2)
+                quantise_pair("o grouped", o_codes, o_planes, j + 1)
+                gated_up(m, 3)
+                norm(j)

@@ -22,7 +22,9 @@ TOKENS = 4 * 576
 TILES = TOKENS // P
 PAIRS = TILES // 2
 LOAD_TILES = 6
-STORE_BANKS = 2
+CHUNKS = TILES * (F // BANK)
+STORE_CHUNKS = 2
+SKEW = 2
 EPS = 1e-5
 
 FLOPS = 2 * TOKENS * D * (D + 2 * F)
@@ -56,10 +58,10 @@ def tile_model_pb_kernel(
 
     with ExitStack() as pools:
         keep = pools.enter_context(tc.tile_pool(name="keep", bufs=1))
-        work = pools.enter_context(tc.tile_pool(name="work", bufs=3))
-        gates = pools.enter_context(tc.tile_pool(name="gates", bufs=4))
+        work = pools.enter_context(tc.tile_pool(name="work", bufs=4))
+        gates = pools.enter_context(tc.tile_pool(name="gates", bufs=8))
         results = pools.enter_context(tc.tile_pool(name="results", bufs=6))
-        banks = pools.enter_context(tc.psum_pool(name="banks", bufs=6))
+        banks = pools.enter_context(tc.psum_pool(name="banks", bufs=3))
         flips = pools.enter_context(tc.psum_pool(name="flips", bufs=2))
 
         o_all = keep.tile([P, TILES, D], BF16)
@@ -116,7 +118,7 @@ def tile_model_pb_kernel(
             columns = slice(half * F, (half + 1) * F)
             nc.sync.dma_start(out=up_codes[:, columns].bitcast(I32), in_=up_words_dram[:, columns])
 
-        gain_bank = banks.tile([P, D], F32, tag="bank")
+        gain_bank = banks.tile([P, D], F32, tag="value")
         nc.tensor.matmul(out=gain_bank[:], lhsT=ones[:], rhs=gain_rows[:], start=True, stop=True)
         gain = keep.tile([P, D], F32)
         nc.scalar.copy(out=gain[:], in_=gain_bank[:])
@@ -156,7 +158,7 @@ def tile_model_pb_kernel(
             if not exists(m):
                 return
             for n in range(2 * m, 2 * m + 2):
-                attn_bank = banks.tile([P, D], F32, tag="bank")
+                attn_bank = banks.tile([P, D], F32, tag="value")
                 nc.tensor.matmul_mx(
                     out=attn_bank[:],
                     lhsT=o_codes[:, n, :].bitcast(FP8X4),
@@ -243,49 +245,65 @@ def tile_model_pb_kernel(
             )
             held[("xn grouped", m)] = grouped
 
-        def gated_up(m, quarter):
-            if not exists(m):
-                return
-            n = 2 * m + quarter // 2
-            part = quarter % 2
-            h_part = results.tile([P, STORE_BANKS, BANK], F32)
-            for b in range(STORE_BANKS):
-                column = (part * STORE_BANKS + b) * BANK
-                gate_bank = banks.tile([P, BANK], F32, tag="bank")
-                value_bank = banks.tile([P, BANK], F32, tag="bank")
-                for u_bank, first in ((gate_bank, column), (value_bank, F + column)):
-                    nc.tensor.matmul_mx(
-                        out=u_bank[:],
-                        lhsT=xn_codes[:, n, :].bitcast(FP8X4),
-                        lhsT_scale=xn_planes[:, n, :],
-                        rhs=up_codes[:, first : first + BANK].bitcast(FP8X4),
-                        rhs_scale=up_plane[:, first : first + BANK],
-                        start=True,
-                        stop=True,
-                    )
-                gate = gates.tile([P, BANK], F32)
-                nc.scalar.activation(out=gate[:], in_=gate_bank[:], func=ACT.Silu)
-                nc.vector.tensor_tensor(
-                    out=h_part[:, b, :], in0=value_bank[:], in1=gate[:], op=ALU.mult
-                )
-            width = STORE_BANKS * BANK
-            nc.sync.dma_start(
-                out=h_dram[:, n, part * width : (part + 1) * width],
-                in_=h_part[:].rearrange("p b c -> p (b c)"),
+        def up_pass(u_bank, c, first):
+            n = c // (F // BANK)
+            nc.tensor.matmul_mx(
+                out=u_bank[:],
+                lhsT=xn_codes[:, n, :].bitcast(FP8X4),
+                lhsT_scale=xn_planes[:, n, :],
+                rhs=up_codes[:, first : first + BANK].bitcast(FP8X4),
+                rhs_scale=up_plane[:, first : first + BANK],
+                start=True,
+                stop=True,
             )
 
+        def gate_half(c):
+            if not 0 <= c < CHUNKS:
+                return
+            gate_bank = banks.tile([P, BANK], F32, tag="gate")
+            up_pass(gate_bank, c, (c % (F // BANK)) * BANK)
+            gate = gates.tile([P, BANK], F32)
+            nc.scalar.activation(out=gate[:], in_=gate_bank[:], func=ACT.Silu)
+            held[("gate", c)] = gate
+
+        def value_half(c):
+            if not 0 <= c < CHUNKS:
+                return
+            value_bank = banks.tile([P, BANK], F32, tag="value")
+            up_pass(value_bank, c, F + (c % (F // BANK)) * BANK)
+            b = c % STORE_CHUNKS
+            if b == 0:
+                h_part = results.tile([P, STORE_CHUNKS, BANK], F32)
+                held["h part"] = h_part
+            h_part = held["h part"]
+            nc.vector.tensor_tensor(
+                out=h_part[:, b, :], in0=value_bank[:], in1=held[("gate", c)][:], op=ALU.mult
+            )
+            if b == STORE_CHUNKS - 1:
+                n = c // (F // BANK)
+                last = (c % (F // BANK) + 1) * BANK
+                nc.sync.dma_start(
+                    out=h_dram[:, n, last - STORE_CHUNKS * BANK : last],
+                    in_=h_part[:].rearrange("p b c -> p (b c)"),
+                )
+
+        def gated_up(m, quarter):
+            for c in range(8 * m + 2 * quarter, 8 * m + 2 * quarter + 2):
+                gate_half(c + SKEW)
+                value_half(c)
+
         with tc.manual_schedule():
-            for j in range(-1, 2 * PAIRS):
-                m = j - PAIRS
-                flip_attention(j + 1)
+            for j in range(-2, 2 * PAIRS + 1):
+                m = j - PAIRS - 1
+                flip_attention(j + 2)
                 project(j)
                 gated_up(m, 0)
                 group_normed(m + 1)
                 gated_up(m, 1)
-                add_residual(j)
+                add_residual(j - 1)
                 flip_normed(m + 2)
                 quantise_pair("xn grouped", xn_codes, xn_planes, m + 1)
                 gated_up(m, 2)
                 quantise_pair("o grouped", o_codes, o_planes, j + 1)
                 gated_up(m, 3)
-                norm(j)
+                norm(j - 1)

@@ -21,10 +21,13 @@ BANK = 512
 TOKENS = 4 * 576
 TILES = TOKENS // P
 PAIRS = TILES // 2
-LOAD_TILES = 6
-CHUNKS = TILES * (F // BANK)
+TILE_CHUNKS = F // BANK
+PAIR_CHUNKS = 2 * TILE_CHUNKS
+CHUNKS = TILES * TILE_CHUNKS
 STORE_CHUNKS = 2
 SKEW = 2
+EARLY_LOADS = (0, 2, 4, 10)
+VECTOR_PAIRS = 2
 EPS = 1e-5
 
 FLOPS = 2 * TOKENS * D * (D + 2 * F)
@@ -61,8 +64,7 @@ def tile_model_pb_kernel(
         work = pools.enter_context(tc.tile_pool(name="work", bufs=4))
         gates = pools.enter_context(tc.tile_pool(name="gates", bufs=8))
         results = pools.enter_context(tc.tile_pool(name="results", bufs=6))
-        banks = pools.enter_context(tc.psum_pool(name="banks", bufs=3))
-        flips = pools.enter_context(tc.psum_pool(name="flips", bufs=2))
+        banks = pools.enter_context(tc.psum_pool(name="banks", bufs=4))
 
         o_all = keep.tile([P, TILES, D], BF16)
         xm_all = keep.tile([P, TILES, D], BF16)
@@ -86,8 +88,6 @@ def tile_model_pb_kernel(
         nc.vector.memset(up_plane[:].bitcast(I32), 0)
         ident_f32 = keep.tile([P, P], F32)
         make_identity(nc, ident_f32[:])
-        ident_bf16 = keep.tile([P, P], BF16)
-        make_identity(nc, ident_bf16[:])
         ones = keep.tile([P, P], BF16)
         nc.gpsimd.memset(ones[:], 1.0)
         minus_half = keep.tile([P, 2], F32)
@@ -97,28 +97,29 @@ def tile_model_pb_kernel(
         nc.vector.memset(warm_in[:], 0.0)
         nc.scalar.activation(out=warm_out[:], in_=warm_in[:], func=ACT.Silu)
 
-        def load_tokens(sbuf, dram, first):
-            tiles = slice(first, first + LOAD_TILES)
-            nc.sync.dma_start(out=sbuf[:, tiles, :], in_=dram[:, tiles, :])
+        def load_tokens(sbuf, dram, first, end):
+            nc.sync.dma_start(out=sbuf[:, first:end, :], in_=dram[:, first:end, :])
 
-        load_tokens(o_all, o_dram, 0)
+        load_tokens(o_all, o_dram, EARLY_LOADS[0], EARLY_LOADS[1])
         nc.sync.dma_start(out=gain_rows[0:1, :], in_=ffn_norm_w.rearrange("(o d) -> o d", o=1))
         load_scale_rows(nc, wo_plane, attn_o_w_scales)
+        load_scale_rows(nc, up_plane, ffn_up_w_scales)
         nc.sync.dma_start(
             out=wo_codes[:].bitcast(I32),
             in_=attn_o_w_words[0].rearrange("p n t -> p (n t)").bitcast(I32),
         )
-        load_scale_rows(nc, up_plane, ffn_up_w_scales)
-        load_tokens(xm_all, xm_dram, 0)
-        for first in range(LOAD_TILES, TILES, LOAD_TILES):
-            load_tokens(o_all, o_dram, first)
-            load_tokens(xm_all, xm_dram, first)
+        load_tokens(xm_all, xm_dram, EARLY_LOADS[0], EARLY_LOADS[1])
+        for first, end in zip(EARLY_LOADS[1:-1], EARLY_LOADS[2:]):
+            load_tokens(o_all, o_dram, first, end)
+            load_tokens(xm_all, xm_dram, first, end)
         up_words_dram = ffn_up_w_words[0].rearrange("p n t -> p (n t)").bitcast(I32)
         for half in range(2):
             columns = slice(half * F, (half + 1) * F)
             nc.sync.dma_start(out=up_codes[:, columns].bitcast(I32), in_=up_words_dram[:, columns])
+        load_tokens(o_all, o_dram, EARLY_LOADS[-1], TILES)
+        load_tokens(xm_all, xm_dram, EARLY_LOADS[-1], TILES)
 
-        gain_bank = banks.tile([P, D], F32, tag="value")
+        gain_bank = banks.tile([P, D], F32, tag="scalar")
         nc.tensor.matmul(out=gain_bank[:], lhsT=ones[:], rhs=gain_rows[:], start=True, stop=True)
         gain = keep.tile([P, D], F32)
         nc.scalar.copy(out=gain[:], in_=gain_bank[:])
@@ -128,37 +129,43 @@ def tile_model_pb_kernel(
         def exists(m):
             return 0 <= m < PAIRS
 
-        def quantise_pair(name, codes, planes, m):
+        def flip(name, source, m):
+            if not exists(m):
+                return
+            words = source[:].bitcast(F32)
+            flipped = banks.tile([P, 2, 2, P], F32, tag="scalar")
+            for a in range(2):
+                for u in range(2):
+                    nc.tensor.transpose(
+                        flipped[:, a, u, :], words[:, 2 * m + a, u : D // 2 : 2], ident_f32[:]
+                    )
+            held[(name, "flipped", m)] = flipped
+
+        def group(name, m):
+            if not exists(m):
+                return
+            grouped = work.tile([P, 2, P, PACK], BF16, tag="grouped", align_bytes=64)
+            nc.scalar.copy(
+                out=grouped[:].bitcast(F32),
+                in_=held[(name, "flipped", m)][:].rearrange("p a u r -> p a r u"),
+            )
+            held[(name, "grouped", m)] = grouped
+
+        def quantise(name, codes, planes, m):
             if not exists(m):
                 return
             pair = slice(2 * m, 2 * m + 2)
             nc.vector.quantize_mx(
                 out=codes[:, pair, :].rearrange("p a r -> p (a r)").bitcast(FP8X4),
                 scales=planes[:, pair, :].rearrange("p a r -> p (a r)"),
-                in_=held[(name, m)][:].rearrange("p a r t -> p (a r t)"),
+                in_=held[(name, "grouped", m)][:].rearrange("p a r t -> p (a r t)"),
             )
-
-        def flip_attention(m):
-            if not exists(m):
-                return
-            o_words = o_all[:].bitcast(F32)
-            flipped = flips.tile([P, 2, 2, P], F32, tag="flip")
-            for a in range(2):
-                for u in range(2):
-                    nc.tensor.transpose(
-                        flipped[:, a, u, :], o_words[:, 2 * m + a, u : D // 2 : 2], ident_f32[:]
-                    )
-            grouped = work.tile([P, 2, P, PACK], BF16, tag="grouped", align_bytes=64)
-            nc.scalar.copy(
-                out=grouped[:].bitcast(F32), in_=flipped[:].rearrange("p a u r -> p a r u")
-            )
-            held[("o grouped", m)] = grouped
 
         def project(m):
             if not exists(m):
                 return
             for n in range(2 * m, 2 * m + 2):
-                attn_bank = banks.tile([P, D], F32, tag="value")
+                attn_bank = banks.tile([P, D], F32, tag="vector")
                 nc.tensor.matmul_mx(
                     out=attn_bank[:],
                     lhsT=o_codes[:, n, :].bitcast(FP8X4),
@@ -183,19 +190,23 @@ def tile_model_pb_kernel(
                 )
             nc.sync.dma_start(out=x2_dram[:, pair, :], in_=x2_all[:, pair, :])
 
+        def mean_square(m, a):
+            if not exists(m):
+                return
+            n = 2 * m + a
+            squares = work.tile([P, D], BF16, tag="squares")
+            nc.scalar.activation(
+                out=squares[:],
+                in_=x2_all[:, n, :],
+                func=ACT.Square,
+                scale=1.0 / math.sqrt(D),
+                accum_out=mean_sq[:, n : n + 1],
+            )
+
         def norm(m):
             if not exists(m):
                 return
             pair = slice(2 * m, 2 * m + 2)
-            for n in range(2 * m, 2 * m + 2):
-                squares = work.tile([P, D], BF16, tag="squares")
-                nc.scalar.activation(
-                    out=squares[:],
-                    in_=x2_all[:, n, :],
-                    func=ACT.Square,
-                    scale=1.0 / math.sqrt(D),
-                    accum_out=mean_sq[:, n : n + 1],
-                )
             nc.gpsimd.tensor_scalar(
                 out=mean_sq_eps[:, pair],
                 in0=mean_sq[:, pair],
@@ -207,6 +218,17 @@ def tile_model_pb_kernel(
             nc.gpsimd.tensor_tensor(
                 out=rstd[:, pair], in0=mean_sq_eps[:, pair], in1=minus_half[:], op=ALU.pow
             )
+            if m < VECTOR_PAIRS:
+                for n in range(2 * m, 2 * m + 2):
+                    nc.vector.scalar_tensor_tensor(
+                        out=xn2_all[:, n, :],
+                        in0=x2_all[:, n, :],
+                        scalar=rstd[:, n : n + 1],
+                        in1=gain[:],
+                        op0=ALU.mult,
+                        op1=ALU.mult,
+                    )
+                return
             scaled = work.tile([P, 2, D], F32, tag="scaled")
             for a in range(2):
                 n = 2 * m + a
@@ -225,28 +247,8 @@ def tile_model_pb_kernel(
                 op=ALU.mult,
             )
 
-        def flip_normed(m):
-            if not exists(m):
-                return
-            flipped = flips.tile([P, 2, PACK, P], BF16, tag="flip")
-            for a in range(2):
-                for t in range(PACK):
-                    nc.tensor.transpose(
-                        flipped[:, a, t, :], xn2_all[:, 2 * m + a, t:D:PACK], ident_bf16[:]
-                    )
-            held[("xn flipped", m)] = flipped
-
-        def group_normed(m):
-            if not exists(m):
-                return
-            grouped = work.tile([P, 2, P, PACK], BF16, tag="grouped", align_bytes=64)
-            nc.scalar.copy(
-                out=grouped[:], in_=held[("xn flipped", m)][:].rearrange("p a t r -> p a r t")
-            )
-            held[("xn grouped", m)] = grouped
-
         def up_pass(u_bank, c, first):
-            n = c // (F // BANK)
+            n = c // TILE_CHUNKS
             nc.tensor.matmul_mx(
                 out=u_bank[:],
                 lhsT=xn_codes[:, n, :].bitcast(FP8X4),
@@ -260,8 +262,8 @@ def tile_model_pb_kernel(
         def gate_half(c):
             if not 0 <= c < CHUNKS:
                 return
-            gate_bank = banks.tile([P, BANK], F32, tag="gate")
-            up_pass(gate_bank, c, (c % (F // BANK)) * BANK)
+            gate_bank = banks.tile([P, BANK], F32, tag="scalar")
+            up_pass(gate_bank, c, (c % TILE_CHUNKS) * BANK)
             gate = gates.tile([P, BANK], F32)
             nc.scalar.activation(out=gate[:], in_=gate_bank[:], func=ACT.Silu)
             held[("gate", c)] = gate
@@ -269,8 +271,8 @@ def tile_model_pb_kernel(
         def value_half(c):
             if not 0 <= c < CHUNKS:
                 return
-            value_bank = banks.tile([P, BANK], F32, tag="value")
-            up_pass(value_bank, c, F + (c % (F // BANK)) * BANK)
+            value_bank = banks.tile([P, BANK], F32, tag="vector")
+            up_pass(value_bank, c, F + (c % TILE_CHUNKS) * BANK)
             b = c % STORE_CHUNKS
             if b == 0:
                 h_part = results.tile([P, STORE_CHUNKS, BANK], F32)
@@ -280,30 +282,34 @@ def tile_model_pb_kernel(
                 out=h_part[:, b, :], in0=value_bank[:], in1=held[("gate", c)][:], op=ALU.mult
             )
             if b == STORE_CHUNKS - 1:
-                n = c // (F // BANK)
-                last = (c % (F // BANK) + 1) * BANK
+                n = c // TILE_CHUNKS
+                last = (c % TILE_CHUNKS + 1) * BANK
                 nc.sync.dma_start(
                     out=h_dram[:, n, last - STORE_CHUNKS * BANK : last],
                     in_=h_part[:].rearrange("p b c -> p (b c)"),
                 )
 
         def gated_up(m, quarter):
-            for c in range(8 * m + 2 * quarter, 8 * m + 2 * quarter + 2):
+            first = PAIR_CHUNKS * m + 2 * quarter
+            for c in range(first, first + 2):
                 gate_half(c + SKEW)
                 value_half(c)
 
         with tc.manual_schedule():
-            for j in range(-2, 2 * PAIRS + 1):
-                m = j - PAIRS - 1
-                flip_attention(j + 2)
-                project(j)
-                gated_up(m, 0)
-                group_normed(m + 1)
-                gated_up(m, 1)
+            for j in range(PAIRS + 4):
+                m = j - 4
+                flip("o", o_all, j)
+                flip("xn", xn2_all, j - 3)
+                project(j - 1)
+                group("o", j)
+                group("xn", j - 3)
                 add_residual(j - 1)
-                flip_normed(m + 2)
-                quantise_pair("xn grouped", xn_codes, xn_planes, m + 1)
+                gated_up(m, 0)
+                quantise("o", o_codes, o_planes, j)
+                quantise("xn", xn_codes, xn_planes, j - 3)
+                gated_up(m, 1)
+                mean_square(j - 1, 0)
                 gated_up(m, 2)
-                quantise_pair("o grouped", o_codes, o_planes, j + 1)
-                gated_up(m, 3)
+                mean_square(j - 1, 1)
                 norm(j - 1)
+                gated_up(m, 3)

@@ -26,8 +26,9 @@ PAIR_CHUNKS = 2 * TILE_CHUNKS
 CHUNKS = TILES * TILE_CHUNKS
 STORE_CHUNKS = 2
 SKEW = 2
-EARLY_LOADS = (0, 2, 4, 10)
-VECTOR_PAIRS = 2
+LEAD = 6
+LOADS_BEFORE_UP = (0, 2, 4, 8, 14)
+VECTOR_PAIRS = 1
 EPS = 1e-5
 
 FLOPS = 2 * TOKENS * D * (D + 2 * F)
@@ -100,24 +101,24 @@ def tile_model_pb_kernel(
         def load_tokens(sbuf, dram, first, end):
             nc.sync.dma_start(out=sbuf[:, first:end, :], in_=dram[:, first:end, :])
 
-        load_tokens(o_all, o_dram, EARLY_LOADS[0], EARLY_LOADS[1])
-        nc.sync.dma_start(out=gain_rows[0:1, :], in_=ffn_norm_w.rearrange("(o d) -> o d", o=1))
-        load_scale_rows(nc, wo_plane, attn_o_w_scales)
-        load_scale_rows(nc, up_plane, ffn_up_w_scales)
+        load_tokens(o_all, o_dram, LOADS_BEFORE_UP[0], LOADS_BEFORE_UP[1])
         nc.sync.dma_start(
             out=wo_codes[:].bitcast(I32),
             in_=attn_o_w_words[0].rearrange("p n t -> p (n t)").bitcast(I32),
         )
-        load_tokens(xm_all, xm_dram, EARLY_LOADS[0], EARLY_LOADS[1])
-        for first, end in zip(EARLY_LOADS[1:-1], EARLY_LOADS[2:]):
+        load_scale_rows(nc, wo_plane, attn_o_w_scales)
+        load_tokens(xm_all, xm_dram, LOADS_BEFORE_UP[0], LOADS_BEFORE_UP[1])
+        nc.sync.dma_start(out=gain_rows[0:1, :], in_=ffn_norm_w.rearrange("(o d) -> o d", o=1))
+        for first, end in zip(LOADS_BEFORE_UP[1:-1], LOADS_BEFORE_UP[2:]):
             load_tokens(o_all, o_dram, first, end)
             load_tokens(xm_all, xm_dram, first, end)
+        load_scale_rows(nc, up_plane, ffn_up_w_scales)
         up_words_dram = ffn_up_w_words[0].rearrange("p n t -> p (n t)").bitcast(I32)
         for half in range(2):
             columns = slice(half * F, (half + 1) * F)
             nc.sync.dma_start(out=up_codes[:, columns].bitcast(I32), in_=up_words_dram[:, columns])
-        load_tokens(o_all, o_dram, EARLY_LOADS[-1], TILES)
-        load_tokens(xm_all, xm_dram, EARLY_LOADS[-1], TILES)
+        load_tokens(o_all, o_dram, LOADS_BEFORE_UP[-1], TILES)
+        load_tokens(xm_all, xm_dram, LOADS_BEFORE_UP[-1], TILES)
 
         gain_bank = banks.tile([P, D], F32, tag="scalar")
         nc.tensor.matmul(out=gain_bank[:], lhsT=ones[:], rhs=gain_rows[:], start=True, stop=True)
@@ -161,39 +162,36 @@ def tile_model_pb_kernel(
                 in_=held[(name, "grouped", m)][:].rearrange("p a r t -> p (a r t)"),
             )
 
-        def project(m):
-            if not exists(m):
+        def project(n):
+            if not 0 <= n < TILES:
                 return
-            for n in range(2 * m, 2 * m + 2):
-                attn_bank = banks.tile([P, D], F32, tag="vector")
-                nc.tensor.matmul_mx(
-                    out=attn_bank[:],
-                    lhsT=o_codes[:, n, :].bitcast(FP8X4),
-                    lhsT_scale=o_planes[:, n, :],
-                    rhs=wo_codes[:].bitcast(FP8X4),
-                    rhs_scale=wo_plane[:],
-                    start=True,
-                    stop=True,
-                )
-                held[("attn bank", n)] = attn_bank
+            attn_bank = banks.tile([P, D], F32, tag="vector")
+            nc.tensor.matmul_mx(
+                out=attn_bank[:],
+                lhsT=o_codes[:, n, :].bitcast(FP8X4),
+                lhsT_scale=o_planes[:, n, :],
+                rhs=wo_codes[:].bitcast(FP8X4),
+                rhs_scale=wo_plane[:],
+                start=True,
+                stop=True,
+            )
+            held[("attn bank", n)] = attn_bank
 
-        def add_residual(m):
-            if not exists(m):
+        def add_residual(n):
+            if not 0 <= n < TILES:
                 return
-            pair = slice(2 * m, 2 * m + 2)
-            for n in range(2 * m, 2 * m + 2):
-                nc.vector.tensor_tensor(
-                    out=x2_all[:, n, :],
-                    in0=held[("attn bank", n)][:],
-                    in1=xm_all[:, n, :],
-                    op=ALU.add,
-                )
-            nc.sync.dma_start(out=x2_dram[:, pair, :], in_=x2_all[:, pair, :])
+            nc.vector.tensor_tensor(
+                out=x2_all[:, n, :],
+                in0=held[("attn bank", n)][:],
+                in1=xm_all[:, n, :],
+                op=ALU.add,
+            )
+            if n % 2 == 1:
+                nc.sync.dma_start(out=x2_dram[:, n - 1 : n + 1, :], in_=x2_all[:, n - 1 : n + 1, :])
 
-        def mean_square(m, a):
-            if not exists(m):
+        def mean_square(n):
+            if not 0 <= n < TILES:
                 return
-            n = 2 * m + a
             squares = work.tile([P, D], BF16, tag="squares")
             nc.scalar.activation(
                 out=squares[:],
@@ -219,15 +217,6 @@ def tile_model_pb_kernel(
                 out=rstd[:, pair], in0=mean_sq_eps[:, pair], in1=minus_half[:], op=ALU.pow
             )
             if m < VECTOR_PAIRS:
-                for n in range(2 * m, 2 * m + 2):
-                    nc.vector.scalar_tensor_tensor(
-                        out=xn2_all[:, n, :],
-                        in0=x2_all[:, n, :],
-                        scalar=rstd[:, n : n + 1],
-                        in1=gain[:],
-                        op0=ALU.mult,
-                        op1=ALU.mult,
-                    )
                 return
             scaled = work.tile([P, 2, D], F32, tag="scaled")
             for a in range(2):
@@ -246,6 +235,19 @@ def tile_model_pb_kernel(
                 in1=gain[:].unsqueeze(1).to_broadcast([P, 2, D]),
                 op=ALU.mult,
             )
+
+        def norm_on_vector(m):
+            if not 0 <= m < VECTOR_PAIRS:
+                return
+            for n in range(2 * m, 2 * m + 2):
+                nc.vector.scalar_tensor_tensor(
+                    out=xn2_all[:, n, :],
+                    in0=x2_all[:, n, :],
+                    scalar=rstd[:, n : n + 1],
+                    in1=gain[:],
+                    op0=ALU.mult,
+                    op1=ALU.mult,
+                )
 
         def up_pass(u_bank, c, first):
             n = c // TILE_CHUNKS
@@ -296,20 +298,23 @@ def tile_model_pb_kernel(
                 value_half(c)
 
         with tc.manual_schedule():
-            for j in range(PAIRS + 4):
-                m = j - 4
-                flip("o", o_all, j)
-                flip("xn", xn2_all, j - 3)
-                project(j - 1)
-                group("o", j)
-                group("xn", j - 3)
-                add_residual(j - 1)
+            for s in range(-2, PAIRS + LEAD):
+                m = s - LEAD
+                project(2 * s)
+                flip("xn", xn2_all, m + 1)
+                flip("o", o_all, s + 2)
+                group("xn", m + 1)
+                group("o", s + 2)
+                add_residual(2 * s)
                 gated_up(m, 0)
-                quantise("o", o_codes, o_planes, j)
-                quantise("xn", xn_codes, xn_planes, j - 3)
+                quantise("o", o_codes, o_planes, s + 1)
+                quantise("xn", xn_codes, xn_planes, m + 1)
                 gated_up(m, 1)
-                mean_square(j - 1, 0)
+                mean_square(2 * s)
+                project(2 * s + 1)
+                add_residual(2 * s + 1)
+                norm_on_vector(s - 2)
                 gated_up(m, 2)
-                mean_square(j - 1, 1)
-                norm(j - 1)
+                mean_square(2 * s + 1)
+                norm(s)
                 gated_up(m, 3)

@@ -28,7 +28,7 @@ STORE_CHUNKS = 2
 SKEW = 2
 LEAD = 6
 LOADS_BEFORE_UP = (0, 2, 4, 8, 14)
-VECTOR_PAIRS = 1
+VECTOR_PAIRS = 3
 EPS = 1e-5
 
 FLOPS = 2 * TOKENS * D * (D + 2 * F)
@@ -201,11 +201,11 @@ def tile_model_pb_kernel(
                 accum_out=mean_sq[:, n : n + 1],
             )
 
-        def norm(m):
+        def start_norm(m):
             if not exists(m):
                 return
             pair = slice(2 * m, 2 * m + 2)
-            nc.gpsimd.tensor_scalar(
+            nc.vector.tensor_scalar(
                 out=mean_sq_eps[:, pair],
                 in0=mean_sq[:, pair],
                 scalar1=1.0,
@@ -216,8 +216,12 @@ def tile_model_pb_kernel(
             nc.gpsimd.tensor_tensor(
                 out=rstd[:, pair], in0=mean_sq_eps[:, pair], in1=minus_half[:], op=ALU.pow
             )
-            if m < VECTOR_PAIRS:
+
+        def norm_on_gpsimd(m):
+            if not VECTOR_PAIRS <= m < PAIRS:
                 return
+            start_norm(m)
+            pair = slice(2 * m, 2 * m + 2)
             scaled = work.tile([P, 2, D], F32, tag="scaled")
             for a in range(2):
                 n = 2 * m + a
@@ -309,6 +313,9 @@ def tile_model_pb_kernel(
                 gated_up(m, 0)
                 quantise("o", o_codes, o_planes, s + 1)
                 quantise("xn", xn_codes, xn_planes, m + 1)
+                if s - 1 < VECTOR_PAIRS:
+                    start_norm(s - 1)
+                norm_on_gpsimd(m + 3)
                 gated_up(m, 1)
                 mean_square(2 * s)
                 project(2 * s + 1)
@@ -316,5 +323,4 @@ def tile_model_pb_kernel(
                 norm_on_vector(s - 2)
                 gated_up(m, 2)
                 mean_square(2 * s + 1)
-                norm(s)
                 gated_up(m, 3)

@@ -26,7 +26,7 @@ PAIR_CHUNKS = 2 * TILE_CHUNKS
 CHUNKS = TILES * TILE_CHUNKS
 STORE_CHUNKS = 2
 SKEW = 2
-LEAD = 6
+LEAD = 5
 LOADS_BEFORE_UP = (0, 2, 4, 8, 14)
 VECTOR_PAIRS = 3
 EPS = 1e-5
@@ -102,6 +102,7 @@ def tile_model_pb_kernel(
             nc.sync.dma_start(out=sbuf[:, first:end, :], in_=dram[:, first:end, :])
 
         load_tokens(o_all, o_dram, LOADS_BEFORE_UP[0], LOADS_BEFORE_UP[1])
+        load_tokens(o_all, o_dram, LOADS_BEFORE_UP[1], LOADS_BEFORE_UP[2])
         nc.sync.dma_start(
             out=wo_codes[:].bitcast(I32),
             in_=attn_o_w_words[0].rearrange("p n t -> p (n t)").bitcast(I32),
@@ -109,7 +110,8 @@ def tile_model_pb_kernel(
         load_scale_rows(nc, wo_plane, attn_o_w_scales)
         load_tokens(xm_all, xm_dram, LOADS_BEFORE_UP[0], LOADS_BEFORE_UP[1])
         nc.sync.dma_start(out=gain_rows[0:1, :], in_=ffn_norm_w.rearrange("(o d) -> o d", o=1))
-        for first, end in zip(LOADS_BEFORE_UP[1:-1], LOADS_BEFORE_UP[2:]):
+        load_tokens(xm_all, xm_dram, LOADS_BEFORE_UP[1], LOADS_BEFORE_UP[2])
+        for first, end in zip(LOADS_BEFORE_UP[2:-1], LOADS_BEFORE_UP[3:]):
             load_tokens(o_all, o_dram, first, end)
             load_tokens(xm_all, xm_dram, first, end)
         load_scale_rows(nc, up_plane, ffn_up_w_scales)
@@ -120,15 +122,19 @@ def tile_model_pb_kernel(
         load_tokens(o_all, o_dram, LOADS_BEFORE_UP[-1], TILES)
         load_tokens(xm_all, xm_dram, LOADS_BEFORE_UP[-1], TILES)
 
-        gain_bank = banks.tile([P, D], F32, tag="scalar")
-        nc.tensor.matmul(out=gain_bank[:], lhsT=ones[:], rhs=gain_rows[:], start=True, stop=True)
-        gain = keep.tile([P, D], F32)
-        nc.scalar.copy(out=gain[:], in_=gain_bank[:])
-
         held = {}
 
         def exists(m):
             return 0 <= m < PAIRS
+
+        gain = keep.tile([P, D], F32)
+
+        def broadcast_gain():
+            gain_bank = banks.tile([P, D], F32, tag="scalar")
+            nc.tensor.matmul(
+                out=gain_bank[:], lhsT=ones[:], rhs=gain_rows[:], start=True, stop=True
+            )
+            nc.scalar.copy(out=gain[:], in_=gain_bank[:])
 
         def flip(name, source, m):
             if not exists(m):
@@ -302,7 +308,13 @@ def tile_model_pb_kernel(
                 value_half(c)
 
         with tc.manual_schedule():
-            for s in range(-2, PAIRS + LEAD):
+            flip("o", o_all, 0)
+            group("o", 0)
+            flip("o", o_all, 1)
+            group("o", 1)
+            quantise("o", o_codes, o_planes, 0)
+            broadcast_gain()
+            for s in range(PAIRS + LEAD):
                 m = s - LEAD
                 project(2 * s)
                 flip("xn", xn2_all, m + 1)

@@ -26,8 +26,7 @@ PAIR_CHUNKS = 2 * TILE_CHUNKS
 CHUNKS = TILES * TILE_CHUNKS
 STORE_CHUNKS = 2
 SKEW = 2
-LEAD = 5
-LOADS_BEFORE_UP = (0, 2, 4, 8, 14)
+LEAD = 4
 VECTOR_PAIRS = 3
 EPS = 1e-5
 
@@ -63,6 +62,7 @@ def tile_model_pb_kernel(
     with ExitStack() as pools:
         keep = pools.enter_context(tc.tile_pool(name="keep", bufs=1))
         work = pools.enter_context(tc.tile_pool(name="work", bufs=4))
+        staged = pools.enter_context(tc.tile_pool(name="staged", bufs=8))
         gates = pools.enter_context(tc.tile_pool(name="gates", bufs=8))
         results = pools.enter_context(tc.tile_pool(name="results", bufs=6))
         banks = pools.enter_context(tc.psum_pool(name="banks", bufs=4))
@@ -101,26 +101,27 @@ def tile_model_pb_kernel(
         def load_tokens(sbuf, dram, first, end):
             nc.sync.dma_start(out=sbuf[:, first:end, :], in_=dram[:, first:end, :])
 
-        load_tokens(o_all, o_dram, LOADS_BEFORE_UP[0], LOADS_BEFORE_UP[1])
-        load_tokens(o_all, o_dram, LOADS_BEFORE_UP[1], LOADS_BEFORE_UP[2])
+        load_tokens(o_all, o_dram, 0, 2)
+        load_tokens(o_all, o_dram, 2, 4)
         nc.sync.dma_start(
             out=wo_codes[:].bitcast(I32),
             in_=attn_o_w_words[0].rearrange("p n t -> p (n t)").bitcast(I32),
         )
         load_scale_rows(nc, wo_plane, attn_o_w_scales)
-        load_tokens(xm_all, xm_dram, LOADS_BEFORE_UP[0], LOADS_BEFORE_UP[1])
+        load_tokens(xm_all, xm_dram, 0, 2)
         nc.sync.dma_start(out=gain_rows[0:1, :], in_=ffn_norm_w.rearrange("(o d) -> o d", o=1))
-        load_tokens(xm_all, xm_dram, LOADS_BEFORE_UP[1], LOADS_BEFORE_UP[2])
-        for first, end in zip(LOADS_BEFORE_UP[2:-1], LOADS_BEFORE_UP[3:]):
-            load_tokens(o_all, o_dram, first, end)
-            load_tokens(xm_all, xm_dram, first, end)
+        load_tokens(o_all, o_dram, 4, 8)
+        load_tokens(xm_all, xm_dram, 2, 4)
+        load_tokens(o_all, o_dram, 8, 12)
+        load_tokens(xm_all, xm_dram, 4, 6)
+        load_tokens(o_all, o_dram, 12, 18)
+        load_tokens(xm_all, xm_dram, 6, 10)
         load_scale_rows(nc, up_plane, ffn_up_w_scales)
         up_words_dram = ffn_up_w_words[0].rearrange("p n t -> p (n t)").bitcast(I32)
         for half in range(2):
             columns = slice(half * F, (half + 1) * F)
             nc.sync.dma_start(out=up_codes[:, columns].bitcast(I32), in_=up_words_dram[:, columns])
-        load_tokens(o_all, o_dram, LOADS_BEFORE_UP[-1], TILES)
-        load_tokens(xm_all, xm_dram, LOADS_BEFORE_UP[-1], TILES)
+        load_tokens(xm_all, xm_dram, 10, 18)
 
         held = {}
 
@@ -151,7 +152,7 @@ def tile_model_pb_kernel(
         def group(name, m):
             if not exists(m):
                 return
-            grouped = work.tile([P, 2, P, PACK], BF16, tag="grouped", align_bytes=64)
+            grouped = staged.tile([P, 2, P, PACK], BF16, tag="grouped", align_bytes=64)
             nc.scalar.copy(
                 out=grouped[:].bitcast(F32),
                 in_=held[(name, "flipped", m)][:].rearrange("p a u r -> p a r u"),
@@ -318,10 +319,13 @@ def tile_model_pb_kernel(
                 m = s - LEAD
                 project(2 * s)
                 flip("xn", xn2_all, m + 1)
-                flip("o", o_all, s + 2)
+                flip("o", o_all, 2 * s + 2)
+                flip("o", o_all, 2 * s + 3)
                 group("xn", m + 1)
-                group("o", s + 2)
+                group("o", 2 * s + 2)
+                group("o", 2 * s + 3)
                 add_residual(2 * s)
+                norm_on_vector(s - 2)
                 gated_up(m, 0)
                 quantise("o", o_codes, o_planes, s + 1)
                 quantise("xn", xn_codes, xn_planes, m + 1)
@@ -332,7 +336,6 @@ def tile_model_pb_kernel(
                 mean_square(2 * s)
                 project(2 * s + 1)
                 add_residual(2 * s + 1)
-                norm_on_vector(s - 2)
                 gated_up(m, 2)
                 mean_square(2 * s + 1)
                 gated_up(m, 3)

@@ -129,6 +129,7 @@ def tile_model_pb_kernel(
             return 0 <= m < PAIRS
 
         gain = keep.tile([P, D], F32)
+        gain_sorted = keep.tile([P, D], F32)
 
         def broadcast_gain():
             gain_bank = banks.tile([P, D], F32, tag="scalar")
@@ -136,17 +137,23 @@ def tile_model_pb_kernel(
                 out=gain_bank[:], lhsT=ones[:], rhs=gain_rows[:], start=True, stop=True
             )
             nc.scalar.copy(out=gain[:], in_=gain_bank[:])
+            nc.scalar.copy(
+                out=gain_sorted[:].rearrange("p (u q e) -> p u q e", u=2, e=2),
+                in_=gain_bank[:].rearrange("p (q u e) -> p u q e", u=2, e=2),
+            )
 
-        def flip(name, source, m):
+        def flip(name, source, m, is_sorted=False):
             if not exists(m):
                 return
             words = source[:].bitcast(F32)
             flipped = banks.tile([P, 2, 2, P], F32, tag="scalar")
             for a in range(2):
                 for u in range(2):
-                    nc.tensor.transpose(
-                        flipped[:, a, u, :], words[:, 2 * m + a, u : D // 2 : 2], ident_f32[:]
-                    )
+                    if is_sorted:
+                        chosen = words[:, 2 * m + a, u * P : (u + 1) * P]
+                    else:
+                        chosen = words[:, 2 * m + a, u : D // 2 : 2]
+                    nc.tensor.transpose(flipped[:, a, u, :], chosen, ident_f32[:])
             held[(name, "flipped", m)] = flipped
 
         def group(name, m):
@@ -233,8 +240,8 @@ def tile_model_pb_kernel(
             for a in range(2):
                 n = 2 * m + a
                 nc.gpsimd.tensor_scalar(
-                    out=scaled[:, a, :],
-                    in0=x2_all[:, n, :],
+                    out=scaled[:, a, :].rearrange("p (u q e) -> p u q e", u=2, e=2),
+                    in0=x2_all[:, n, :].rearrange("p (q u e) -> p u q e", u=2, e=2),
                     scalar1=rstd[:, n : n + 1],
                     scalar2=0.0,
                     op0=ALU.mult,
@@ -243,7 +250,7 @@ def tile_model_pb_kernel(
             nc.gpsimd.tensor_tensor(
                 out=xn2_all[:, pair, :],
                 in0=scaled[:],
-                in1=gain[:].unsqueeze(1).to_broadcast([P, 2, D]),
+                in1=gain_sorted[:].unsqueeze(1).to_broadcast([P, 2, D]),
                 op=ALU.mult,
             )
 
@@ -318,7 +325,7 @@ def tile_model_pb_kernel(
             for s in range(PAIRS + LEAD):
                 m = s - LEAD
                 project(2 * s)
-                flip("xn", xn2_all, m + 1)
+                flip("xn", xn2_all, m + 1, is_sorted=m + 1 >= VECTOR_PAIRS)
                 flip("o", o_all, 2 * s + 2)
                 flip("o", o_all, 2 * s + 3)
                 group("xn", m + 1)

@@ -73,12 +73,15 @@ def tile_model_pb_kernel(
         xn2_all = keep.tile([P, TILES, D], BF16)
         wo_codes = keep.tile([P, D], U32, align_bytes=64)
         wo_plane = keep.tile([P, D], U8, align_bytes=64)
-        up_codes = keep.tile([P, 2 * F], U32, align_bytes=64)
-        up_plane = keep.tile([P, 2 * F], U8, align_bytes=64)
+        up_codes = keep.tile([P, 2 * F], U32, align_bytes=256)
+        up_plane_room = keep.tile([P, 192 + 2 * F], U8, align_bytes=256)
+        up_plane = up_plane_room[:, 192:]
         o_codes = keep.tile([P, TILES, P], U32, align_bytes=64)
         o_planes = keep.tile([P, TILES, P], U8, align_bytes=64)
-        xn_codes = keep.tile([P, TILES, P], U32, align_bytes=64)
-        xn_planes = keep.tile([P, TILES, P], U8, align_bytes=64)
+        xn_codes_room = keep.tile([P, 16 + TILES * P], U32, align_bytes=256)
+        xn_codes = xn_codes_room[:, 16:].rearrange("p (n r) -> p n r", r=P)
+        xn_planes_room = keep.tile([P, 128 + TILES * P], U8, align_bytes=256)
+        xn_planes = xn_planes_room[:, 128:].rearrange("p (n r) -> p n r", r=P)
         mean_sq = keep.tile([P, TILES], F32)
         mean_sq_eps = keep.tile([P, TILES], F32)
         rstd = keep.tile([P, TILES], F32)
@@ -86,7 +89,7 @@ def tile_model_pb_kernel(
         gain_rows = keep.tile([P, D], BF16)
         nc.vector.memset(gain_rows[:], 0.0)
         nc.vector.memset(wo_plane[:].bitcast(I32), 0)
-        nc.vector.memset(up_plane[:].bitcast(I32), 0)
+        nc.vector.memset(up_plane_room[:].bitcast(I32), 0)
         ident_f32 = keep.tile([P, P], F32)
         make_identity(nc, ident_f32[:])
         ones = keep.tile([P, P], BF16)
@@ -128,18 +131,19 @@ def tile_model_pb_kernel(
         def exists(m):
             return 0 <= m < PAIRS
 
-        gain = keep.tile([P, D], F32)
         gain_sorted = keep.tile([P, D], F32)
+
+        def sorted_view(row):
+            return row.rearrange("p (q u e) -> p u q e", u=2, e=2)
 
         def broadcast_gain():
             gain_bank = banks.tile([P, D], F32, tag="scalar")
             nc.tensor.matmul(
                 out=gain_bank[:], lhsT=ones[:], rhs=gain_rows[:], start=True, stop=True
             )
-            nc.scalar.copy(out=gain[:], in_=gain_bank[:])
             nc.scalar.copy(
                 out=gain_sorted[:].rearrange("p (u q e) -> p u q e", u=2, e=2),
-                in_=gain_bank[:].rearrange("p (q u e) -> p u q e", u=2, e=2),
+                in_=sorted_view(gain_bank[:]),
             )
 
         def flip(name, source, m, is_sorted=False):
@@ -241,7 +245,7 @@ def tile_model_pb_kernel(
                 n = 2 * m + a
                 nc.gpsimd.tensor_scalar(
                     out=scaled[:, a, :].rearrange("p (u q e) -> p u q e", u=2, e=2),
-                    in0=x2_all[:, n, :].rearrange("p (q u e) -> p u q e", u=2, e=2),
+                    in0=sorted_view(x2_all[:, n, :]),
                     scalar1=rstd[:, n : n + 1],
                     scalar2=0.0,
                     op0=ALU.mult,
@@ -258,14 +262,16 @@ def tile_model_pb_kernel(
             if not 0 <= m < VECTOR_PAIRS:
                 return
             for n in range(2 * m, 2 * m + 2):
-                nc.vector.scalar_tensor_tensor(
-                    out=xn2_all[:, n, :],
-                    in0=x2_all[:, n, :],
-                    scalar=rstd[:, n : n + 1],
-                    in1=gain[:],
-                    op0=ALU.mult,
-                    op1=ALU.mult,
-                )
+                for u in range(2):
+                    half = slice(u * (D // 2), (u + 1) * (D // 2))
+                    nc.vector.scalar_tensor_tensor(
+                        out=xn2_all[:, n, half].rearrange("p (q e) -> p q e", e=2),
+                        in0=sorted_view(x2_all[:, n, :])[:, u, :, :],
+                        scalar=rstd[:, n : n + 1],
+                        in1=gain_sorted[:, half].rearrange("p (q e) -> p q e", e=2),
+                        op0=ALU.mult,
+                        op1=ALU.mult,
+                    )
 
         def up_pass(u_bank, c, first):
             n = c // TILE_CHUNKS
@@ -325,7 +331,7 @@ def tile_model_pb_kernel(
             for s in range(PAIRS + LEAD):
                 m = s - LEAD
                 project(2 * s)
-                flip("xn", xn2_all, m + 1, is_sorted=m + 1 >= VECTOR_PAIRS)
+                flip("xn", xn2_all, m + 1, is_sorted=True)
                 flip("o", o_all, 2 * s + 2)
                 flip("o", o_all, 2 * s + 3)
                 group("xn", m + 1)

@@ -28,6 +28,8 @@ STORE_CHUNKS = 2
 SKEW = 2
 LEAD = 4
 VECTOR_PAIRS = 3
+WARM_FIRST = 3
+WARM_STEP = 2
 EPS = 1e-5
 
 FLOPS = 2 * TOKENS * D * (D + 2 * F)
@@ -90,10 +92,12 @@ def tile_model_pb_kernel(
         nc.vector.memset(gain_rows[:], 0.0)
         nc.vector.memset(wo_plane[:].bitcast(I32), 0)
         nc.vector.memset(up_plane_room[:].bitcast(I32), 0)
-        ident_f32 = keep.tile([P, P], F32)
-        make_identity(nc, ident_f32[:])
         ones = keep.tile([P, P], BF16)
         nc.gpsimd.memset(ones[:], 1.0)
+        idle_rhs = keep.tile([P, BANK], BF16)
+        nc.gpsimd.memset(idle_rhs[:], 0.0)
+        ident_f32 = keep.tile([P, P], F32)
+        make_identity(nc, ident_f32[:])
         minus_half = keep.tile([P, 2], F32)
         nc.gpsimd.memset(minus_half[:], -0.5)
         warm_in = keep.tile([P, 1], F32)
@@ -132,6 +136,13 @@ def tile_model_pb_kernel(
             return 0 <= m < PAIRS
 
         gain_sorted = keep.tile([P, D], F32)
+
+        def keep_warm(count):
+            for i in range(count):
+                idle_bank = banks.tile([P, BANK], F32, tag="vector")
+                nc.tensor.matmul(
+                    out=idle_bank[:], lhsT=ones[:], rhs=idle_rhs[:], start=True, stop=True
+                )
 
         def sorted_view(row):
             return row.rearrange("p (q u e) -> p u q e", u=2, e=2)
@@ -322,6 +333,7 @@ def tile_model_pb_kernel(
                 value_half(c)
 
         with tc.manual_schedule():
+            keep_warm(WARM_FIRST)
             flip("o", o_all, 0)
             group("o", 0)
             flip("o", o_all, 1)
@@ -349,6 +361,8 @@ def tile_model_pb_kernel(
                 mean_square(2 * s)
                 project(2 * s + 1)
                 add_residual(2 * s + 1)
+                if m < 0:
+                    keep_warm(WARM_STEP)
                 gated_up(m, 2)
                 mean_square(2 * s + 1)
                 gated_up(m, 3)

@@ -339,6 +339,7 @@ def tile_model_pb_kernel(
             flip("o", o_all, 1)
             group("o", 1)
             quantise("o", o_codes, o_planes, 0)
+            keep_warm(WARM_STEP)
             broadcast_gain()
             for s in range(PAIRS + LEAD):
                 m = s - LEAD
@@ -361,7 +362,7 @@ def tile_model_pb_kernel(
                 mean_square(2 * s)
                 project(2 * s + 1)
                 add_residual(2 * s + 1)
-                if m < 0:
+                if -2 <= m < 0:
                     keep_warm(WARM_STEP)
                 gated_up(m, 2)
                 mean_square(2 * s + 1)

@@ -110,13 +110,13 @@ def tile_model_pb_kernel(
 
         load_tokens(o_all, o_dram, 0, 2)
         load_tokens(o_all, o_dram, 2, 4)
+        nc.sync.dma_start(out=gain_rows[0:1, :], in_=ffn_norm_w.rearrange("(o d) -> o d", o=1))
         nc.sync.dma_start(
             out=wo_codes[:].bitcast(I32),
             in_=attn_o_w_words[0].rearrange("p n t -> p (n t)").bitcast(I32),
         )
         load_scale_rows(nc, wo_plane, attn_o_w_scales)
         load_tokens(xm_all, xm_dram, 0, 2)
-        nc.sync.dma_start(out=gain_rows[0:1, :], in_=ffn_norm_w.rearrange("(o d) -> o d", o=1))
         load_tokens(o_all, o_dram, 4, 8)
         load_tokens(xm_all, xm_dram, 2, 4)
         load_tokens(o_all, o_dram, 8, 12)
@@ -339,18 +339,23 @@ def tile_model_pb_kernel(
             flip("o", o_all, 1)
             group("o", 1)
             quantise("o", o_codes, o_planes, 0)
-            keep_warm(WARM_STEP)
             broadcast_gain()
             for s in range(PAIRS + LEAD):
                 m = s - LEAD
                 project(2 * s)
+                if m < 0:
+                    project(2 * s + 1)
                 flip("xn", xn2_all, m + 1, is_sorted=True)
                 flip("o", o_all, 2 * s + 2)
                 flip("o", o_all, 2 * s + 3)
+                add_residual(2 * s)
+                if s == 0:
+                    add_residual(2 * s + 1)
+                    mean_square(2 * s)
+                    mean_square(2 * s + 1)
                 group("xn", m + 1)
                 group("o", 2 * s + 2)
                 group("o", 2 * s + 3)
-                add_residual(2 * s)
                 norm_on_vector(s - 2)
                 gated_up(m, 0)
                 quantise("o", o_codes, o_planes, s + 1)
@@ -359,11 +364,17 @@ def tile_model_pb_kernel(
                     start_norm(s - 1)
                 norm_on_gpsimd(m + 3)
                 gated_up(m, 1)
-                mean_square(2 * s)
-                project(2 * s + 1)
-                add_residual(2 * s + 1)
+                if s > 0:
+                    mean_square(2 * s)
+                if m >= 0:
+                    project(2 * s + 1)
+                if s > 0:
+                    add_residual(2 * s + 1)
                 if -2 <= m < 0:
                     keep_warm(WARM_STEP)
                 gated_up(m, 2)
-                mean_square(2 * s + 1)
+                if 0 < s < LEAD:
+                    mean_square(2 * s + 1)
                 gated_up(m, 3)
+                if m >= 0:
+                    mean_square(2 * s + 1)

@@ -30,6 +30,8 @@ LEAD = 4
 VECTOR_PAIRS = 3
 WARM_FIRST = 3
 WARM_STEP = 2
+END_CHUNKS = 1
+END_PIECES = 2
 EPS = 1e-5
 
 FLOPS = 2 * TOKENS * D * (D + 2 * F)
@@ -284,42 +286,62 @@ def tile_model_pb_kernel(
                         op1=ALU.mult,
                     )
 
-        def up_pass(u_bank, c, first):
+        def up_pass(u_columns, c, first):
             n = c // TILE_CHUNKS
+            width = u_columns.shape[1]
             nc.tensor.matmul_mx(
-                out=u_bank[:],
+                out=u_columns,
                 lhsT=xn_codes[:, n, :].bitcast(FP8X4),
                 lhsT_scale=xn_planes[:, n, :],
-                rhs=up_codes[:, first : first + BANK].bitcast(FP8X4),
-                rhs_scale=up_plane[:, first : first + BANK],
+                rhs=up_codes[:, first : first + width].bitcast(FP8X4),
+                rhs_scale=up_plane[:, first : first + width],
                 start=True,
                 stop=True,
             )
+
+        def pieces(c):
+            count = END_PIECES if c >= CHUNKS - END_CHUNKS else 1
+            width = BANK // count
+            return [slice(i * width, (i + 1) * width) for i in range(count)]
 
         def gate_half(c):
             if not 0 <= c < CHUNKS:
                 return
             gate_bank = banks.tile([P, BANK], F32, tag="scalar")
-            up_pass(gate_bank, c, (c % TILE_CHUNKS) * BANK)
             gate = gates.tile([P, BANK], F32)
-            nc.scalar.activation(out=gate[:], in_=gate_bank[:], func=ACT.Silu)
+            for columns in pieces(c):
+                up_pass(gate_bank[:, columns], c, (c % TILE_CHUNKS) * BANK + columns.start)
+            for columns in pieces(c):
+                nc.scalar.activation(out=gate[:, columns], in_=gate_bank[:, columns], func=ACT.Silu)
             held[("gate", c)] = gate
 
         def value_half(c):
             if not 0 <= c < CHUNKS:
                 return
             value_bank = banks.tile([P, BANK], F32, tag="vector")
-            up_pass(value_bank, c, F + (c % TILE_CHUNKS) * BANK)
+            for columns in pieces(c):
+                up_pass(value_bank[:, columns], c, F + (c % TILE_CHUNKS) * BANK + columns.start)
             b = c % STORE_CHUNKS
             if b == 0:
                 h_part = results.tile([P, STORE_CHUNKS, BANK], F32)
                 held["h part"] = h_part
             h_part = held["h part"]
-            nc.vector.tensor_tensor(
-                out=h_part[:, b, :], in0=value_bank[:], in1=held[("gate", c)][:], op=ALU.mult
-            )
-            if b == STORE_CHUNKS - 1:
-                n = c // TILE_CHUNKS
+            n = c // TILE_CHUNKS
+            at_end = c >= CHUNKS - STORE_CHUNKS
+            for columns in pieces(c):
+                nc.vector.tensor_tensor(
+                    out=h_part[:, b, columns],
+                    in0=value_bank[:, columns],
+                    in1=held[("gate", c)][:, columns],
+                    op=ALU.mult,
+                )
+                if at_end:
+                    first = (c % TILE_CHUNKS) * BANK + columns.start
+                    nc.sync.dma_start(
+                        out=h_dram[:, n, first : first + columns.stop - columns.start],
+                        in_=h_part[:, b, columns],
+                    )
+            if b == STORE_CHUNKS - 1 and not at_end:
                 last = (c % TILE_CHUNKS + 1) * BANK
                 nc.sync.dma_start(
                     out=h_dram[:, n, last - STORE_CHUNKS * BANK : last],

@@ -105,6 +105,7 @@ def tile_model_pb_kernel(
         warm_in = keep.tile([P, 1], F32)
         warm_out = keep.tile([P, 1], F32)
         nc.vector.memset(warm_in[:], 0.0)
+        nc.scalar.dma_start(out=gain_rows[0:1, :], in_=ffn_norm_w.rearrange("(o d) -> o d", o=1))
         nc.scalar.activation(out=warm_out[:], in_=warm_in[:], func=ACT.Silu)
 
         def load_tokens(sbuf, dram, first, end):
@@ -112,7 +113,6 @@ def tile_model_pb_kernel(
 
         load_tokens(o_all, o_dram, 0, 2)
         load_tokens(o_all, o_dram, 2, 4)
-        nc.sync.dma_start(out=gain_rows[0:1, :], in_=ffn_norm_w.rearrange("(o d) -> o d", o=1))
         nc.sync.dma_start(
             out=wo_codes[:].bitcast(I32),
             in_=attn_o_w_words[0].rearrange("p n t -> p (n t)").bitcast(I32),
@@ -362,6 +362,7 @@ def tile_model_pb_kernel(
             group("o", 1)
             quantise("o", o_codes, o_planes, 0)
             broadcast_gain()
+            keep_warm(WARM_STEP)
             for s in range(PAIRS + LEAD):
                 m = s - LEAD
                 project(2 * s)

@@ -105,13 +105,13 @@ def tile_model_pb_kernel(
         warm_in = keep.tile([P, 1], F32)
         warm_out = keep.tile([P, 1], F32)
         nc.vector.memset(warm_in[:], 0.0)
-        nc.scalar.dma_start(out=gain_rows[0:1, :], in_=ffn_norm_w.rearrange("(o d) -> o d", o=1))
         nc.scalar.activation(out=warm_out[:], in_=warm_in[:], func=ACT.Silu)
 
         def load_tokens(sbuf, dram, first, end):
             nc.sync.dma_start(out=sbuf[:, first:end, :], in_=dram[:, first:end, :])
 
-        load_tokens(o_all, o_dram, 0, 2)
+        load_tokens(o_all, o_dram, 0, 1)
+        load_tokens(o_all, o_dram, 1, 2)
         load_tokens(o_all, o_dram, 2, 4)
         nc.sync.dma_start(
             out=wo_codes[:].bitcast(I32),
@@ -120,6 +120,7 @@ def tile_model_pb_kernel(
         load_scale_rows(nc, wo_plane, attn_o_w_scales)
         load_tokens(xm_all, xm_dram, 0, 2)
         load_tokens(o_all, o_dram, 4, 8)
+        nc.sync.dma_start(out=gain_rows[0:1, :], in_=ffn_norm_w.rearrange("(o d) -> o d", o=1))
         load_tokens(xm_all, xm_dram, 2, 4)
         load_tokens(o_all, o_dram, 8, 12)
         load_tokens(xm_all, xm_dram, 4, 6)
@@ -150,11 +151,11 @@ def tile_model_pb_kernel(
             return row.rearrange("p (q u e) -> p u q e", u=2, e=2)
 
         def broadcast_gain():
-            gain_bank = banks.tile([P, D], F32, tag="scalar")
+            gain_bank = banks.tile([P, D], F32, tag="vector")
             nc.tensor.matmul(
                 out=gain_bank[:], lhsT=ones[:], rhs=gain_rows[:], start=True, stop=True
             )
-            nc.scalar.copy(
+            nc.vector.tensor_copy(
                 out=gain_sorted[:].rearrange("p (u q e) -> p u q e", u=2, e=2),
                 in_=sorted_view(gain_bank[:]),
             )
@@ -173,25 +174,32 @@ def tile_model_pb_kernel(
                     nc.tensor.transpose(flipped[:, a, u, :], chosen, ident_f32[:])
             held[(name, "flipped", m)] = flipped
 
+        def by_tile(name, m):
+            if name == "o" and m == 0:
+                return [slice(0, 1), slice(1, 2)]
+            return [slice(0, 2)]
+
         def group(name, m):
             if not exists(m):
                 return
             grouped = staged.tile([P, 2, P, PACK], BF16, tag="grouped", align_bytes=64)
-            nc.scalar.copy(
-                out=grouped[:].bitcast(F32),
-                in_=held[(name, "flipped", m)][:].rearrange("p a u r -> p a r u"),
-            )
+            for tiles in by_tile(name, m):
+                nc.scalar.copy(
+                    out=grouped[:, tiles, :, :].bitcast(F32),
+                    in_=held[(name, "flipped", m)][:, tiles, :, :].rearrange("p a u r -> p a r u"),
+                )
             held[(name, "grouped", m)] = grouped
 
         def quantise(name, codes, planes, m):
             if not exists(m):
                 return
-            pair = slice(2 * m, 2 * m + 2)
-            nc.vector.quantize_mx(
-                out=codes[:, pair, :].rearrange("p a r -> p (a r)").bitcast(FP8X4),
-                scales=planes[:, pair, :].rearrange("p a r -> p (a r)"),
-                in_=held[(name, "grouped", m)][:].rearrange("p a r t -> p (a r t)"),
-            )
+            for tiles in by_tile(name, m):
+                pair = slice(2 * m + tiles.start, 2 * m + tiles.stop)
+                nc.vector.quantize_mx(
+                    out=codes[:, pair, :].rearrange("p a r -> p (a r)").bitcast(FP8X4),
+                    scales=planes[:, pair, :].rearrange("p a r -> p (a r)"),
+                    in_=held[(name, "grouped", m)][:, tiles, :, :].rearrange("p a r t -> p (a r t)"),
+                )
 
         def project(n):
             if not 0 <= n < TILES:
@@ -361,7 +369,6 @@ def tile_model_pb_kernel(
             flip("o", o_all, 1)
             group("o", 1)
             quantise("o", o_codes, o_planes, 0)
-            broadcast_gain()
             keep_warm(WARM_STEP)
             for s in range(PAIRS + LEAD):
                 m = s - LEAD
@@ -383,6 +390,8 @@ def tile_model_pb_kernel(
                 gated_up(m, 0)
                 quantise("o", o_codes, o_planes, s + 1)
                 quantise("xn", xn_codes, xn_planes, m + 1)
+                if s == 0:
+                    broadcast_gain()
                 if s - 1 < VECTOR_PAIRS:
                     start_norm(s - 1)
                 norm_on_gpsimd(m + 3)

import math
from contextlib import ExitStack

import concourse.mybir as mybir
from concourse.masks import make_identity

F32 = mybir.dt.float32
BF16 = mybir.dt.bfloat16
I32 = mybir.dt.int32
U32 = mybir.dt.uint32
U8 = mybir.dt.uint8
FP8X4 = mybir.dt.float8_e4m3fn_x4
ALU = mybir.AluOpType
ACT = mybir.ActivationFunctionType

P = 128
PACK = 4
D = 512
F = 2048
BANK = 512
TOKENS = 4 * 576
TILES = TOKENS // P
PAIRS = TILES // 2
TILE_CHUNKS = F // BANK
PAIR_CHUNKS = 2 * TILE_CHUNKS
CHUNKS = TILES * TILE_CHUNKS
STORE_CHUNKS = 2
SKEW = 2
LEAD = 4
VECTOR_PAIRS = 3
WARM_FIRST = 3
WARM_STEP = 2
END_CHUNKS = 1
END_PIECES = 2
EPS = 1e-5

FLOPS = 2 * TOKENS * D * (D + 2 * F)


def load_scale_rows(nc, plane, scales):
    for quadrant in range(4):
        nc.sync.dma_start(
            out=plane[32 * quadrant : 32 * quadrant + 4, :].bitcast(I32),
            in_=scales[0, 4 * quadrant : 4 * quadrant + 4, :].bitcast(I32),
        )


def tile_model_pb_kernel(
    tc,
    o_attn,
    xm,
    attn_o_w_words,
    attn_o_w_scales,
    ffn_norm_w,
    ffn_up_w_words,
    ffn_up_w_scales,
    out_0,
    out_1,
):
    nc = tc.nc
    o_dram = o_attn.flatten_outer_dims().rearrange("(p n) d -> p n d", n=TILES)
    xm_dram = xm.flatten_outer_dims().rearrange("(p n) d -> p n d", n=TILES)
    x2_dram = out_0.flatten_outer_dims().rearrange("(p n) d -> p n d", n=TILES)
    h_dram = out_1.flatten_outer_dims().rearrange("(p n) f -> p n f", n=TILES)

    with ExitStack() as pools:
        keep = pools.enter_context(tc.tile_pool(name="keep", bufs=1))
        work = pools.enter_context(tc.tile_pool(name="work", bufs=4))
        staged = pools.enter_context(tc.tile_pool(name="staged", bufs=8))
        gates = pools.enter_context(tc.tile_pool(name="gates", bufs=8))
        results = pools.enter_context(tc.tile_pool(name="results", bufs=6))
        banks = pools.enter_context(tc.psum_pool(name="banks", bufs=4))

        o_all = keep.tile([P, TILES, D], BF16)
        xm_all = keep.tile([P, TILES, D], BF16)
        x2_all = keep.tile([P, TILES, D], F32)
        xn2_all = keep.tile([P, TILES, D], BF16)
        wo_codes = keep.tile([P, D], U32, align_bytes=64)
        wo_plane = keep.tile([P, D], U8, align_bytes=64)
        up_codes = keep.tile([P, 2 * F], U32, align_bytes=256)
        up_plane_room = keep.tile([P, 192 + 2 * F], U8, align_bytes=256)
        up_plane = up_plane_room[:, 192:]
        o_codes = keep.tile([P, TILES, P], U32, align_bytes=64)
        o_planes = keep.tile([P, TILES, P], U8, align_bytes=64)
        xn_codes_room = keep.tile([P, 16 + TILES * P], U32, align_bytes=256)
        xn_codes = xn_codes_room[:, 16:].rearrange("p (n r) -> p n r", r=P)
        xn_planes_room = keep.tile([P, 128 + TILES * P], U8, align_bytes=256)
        xn_planes = xn_planes_room[:, 128:].rearrange("p (n r) -> p n r", r=P)
        mean_sq = keep.tile([P, TILES], F32)
        mean_sq_eps = keep.tile([P, TILES], F32)
        rstd = keep.tile([P, TILES], F32)

        gain_rows = keep.tile([P, D], BF16)
        nc.vector.memset(gain_rows[:], 0.0)
        nc.vector.memset(wo_plane[:].bitcast(I32), 0)
        nc.vector.memset(up_plane_room[:].bitcast(I32), 0)
        ones = keep.tile([P, P], BF16)
        nc.gpsimd.memset(ones[:], 1.0)
        idle_rhs = keep.tile([P, BANK], BF16)
        nc.gpsimd.memset(idle_rhs[:], 0.0)
        ident_f32 = keep.tile([P, P], F32)
        make_identity(nc, ident_f32[:])
        minus_half = keep.tile([P, 2], F32)
        nc.gpsimd.memset(minus_half[:], -0.5)
        warm_in = keep.tile([P, 1], F32)
        warm_out = keep.tile([P, 1], F32)
        nc.vector.memset(warm_in[:], 0.0)
        nc.scalar.activation(out=warm_out[:], in_=warm_in[:], func=ACT.Silu)

        def load_tokens(sbuf, dram, first, end):
            nc.sync.dma_start(out=sbuf[:, first:end, :], in_=dram[:, first:end, :])

        load_tokens(o_all, o_dram, 0, 1)
        load_tokens(o_all, o_dram, 1, 2)
        load_tokens(o_all, o_dram, 2, 4)
        nc.sync.dma_start(
            out=wo_codes[:].bitcast(I32),
            in_=attn_o_w_words[0].rearrange("p n t -> p (n t)").bitcast(I32),
        )
        load_scale_rows(nc, wo_plane, attn_o_w_scales)
        load_tokens(xm_all, xm_dram, 0, 2)
        load_tokens(o_all, o_dram, 4, 8)
        nc.sync.dma_start(out=gain_rows[0:1, :], in_=ffn_norm_w.rearrange("(o d) -> o d", o=1))
        load_tokens(xm_all, xm_dram, 2, 4)
        load_tokens(o_all, o_dram, 8, 12)
        load_tokens(xm_all, xm_dram, 4, 6)
        load_tokens(o_all, o_dram, 12, 18)
        load_tokens(xm_all, xm_dram, 6, 10)
        load_scale_rows(nc, up_plane, ffn_up_w_scales)
        up_words_dram = ffn_up_w_words[0].rearrange("p n t -> p (n t)").bitcast(I32)
        for half in range(2):
            columns = slice(half * F, (half + 1) * F)
            nc.sync.dma_start(out=up_codes[:, columns].bitcast(I32), in_=up_words_dram[:, columns])
        load_tokens(xm_all, xm_dram, 10, 18)

        held = {}

        def exists(m):
            return 0 <= m < PAIRS

        gain_sorted = keep.tile([P, D], F32)

        def keep_warm(count):
            for i in range(count):
                idle_bank = banks.tile([P, BANK], F32, tag="vector")
                nc.tensor.matmul(
                    out=idle_bank[:], lhsT=ones[:], rhs=idle_rhs[:], start=True, stop=True
                )

        def sorted_view(row):
            return row.rearrange("p (q u e) -> p u q e", u=2, e=2)

        def broadcast_gain():
            gain_bank = banks.tile([P, D], F32, tag="vector")
            nc.tensor.matmul(
                out=gain_bank[:], lhsT=ones[:], rhs=gain_rows[:], start=True, stop=True
            )
            nc.vector.tensor_copy(
                out=gain_sorted[:].rearrange("p (u q e) -> p u q e", u=2, e=2),
                in_=sorted_view(gain_bank[:]),
            )

        def flip(name, source, m, is_sorted=False):
            if not exists(m):
                return
            words = source[:].bitcast(F32)
            flipped = banks.tile([P, 2, 2, P], F32, tag="scalar")
            for a in range(2):
                for u in range(2):
                    if is_sorted:
                        chosen = words[:, 2 * m + a, u * P : (u + 1) * P]
                    else:
                        chosen = words[:, 2 * m + a, u : D // 2 : 2]
                    nc.tensor.transpose(flipped[:, a, u, :], chosen, ident_f32[:])
            held[(name, "flipped", m)] = flipped

        def by_tile(name, m):
            if name == "o" and m == 0:
                return [slice(0, 1), slice(1, 2)]
            return [slice(0, 2)]

        def group(name, m):
            if not exists(m):
                return
            grouped = staged.tile([P, 2, P, PACK], BF16, tag="grouped", align_bytes=64)
            for tiles in by_tile(name, m):
                nc.scalar.copy(
                    out=grouped[:, tiles, :, :].bitcast(F32),
                    in_=held[(name, "flipped", m)][:, tiles, :, :].rearrange("p a u r -> p a r u"),
                )
            held[(name, "grouped", m)] = grouped

        def quantise(name, codes, planes, m):
            if not exists(m):
                return
            for tiles in by_tile(name, m):
                pair = slice(2 * m + tiles.start, 2 * m + tiles.stop)
                nc.vector.quantize_mx(
                    out=codes[:, pair, :].rearrange("p a r -> p (a r)").bitcast(FP8X4),
                    scales=planes[:, pair, :].rearrange("p a r -> p (a r)"),
                    in_=held[(name, "grouped", m)][:, tiles, :, :].rearrange("p a r t -> p (a r t)"),
                )

        def project(n):
            if not 0 <= n < TILES:
                return
            attn_bank = banks.tile([P, D], F32, tag="vector")
            nc.tensor.matmul_mx(
                out=attn_bank[:],
                lhsT=o_codes[:, n, :].bitcast(FP8X4),
                lhsT_scale=o_planes[:, n, :],
                rhs=wo_codes[:].bitcast(FP8X4),
                rhs_scale=wo_plane[:],
                start=True,
                stop=True,
            )
            held[("attn bank", n)] = attn_bank

        def add_residual(n):
            if not 0 <= n < TILES:
                return
            nc.vector.tensor_tensor(
                out=x2_all[:, n, :],
                in0=held[("attn bank", n)][:],
                in1=xm_all[:, n, :],
                op=ALU.add,
            )
            if n % 2 == 1:
                nc.sync.dma_start(out=x2_dram[:, n - 1 : n + 1, :], in_=x2_all[:, n - 1 : n + 1, :])

        def mean_square(n):
            if not 0 <= n < TILES:
                return
            squares = work.tile([P, D], BF16, tag="squares")
            nc.scalar.activation(
                out=squares[:],
                in_=x2_all[:, n, :],
                func=ACT.Square,
                scale=1.0 / math.sqrt(D),
                accum_out=mean_sq[:, n : n + 1],
            )

        def start_norm(m):
            if not exists(m):
                return
            pair = slice(2 * m, 2 * m + 2)
            nc.vector.tensor_scalar(
                out=mean_sq_eps[:, pair],
                in0=mean_sq[:, pair],
                scalar1=1.0,
                scalar2=EPS,
                op0=ALU.mult,
                op1=ALU.add,
            )
            nc.gpsimd.tensor_tensor(
                out=rstd[:, pair], in0=mean_sq_eps[:, pair], in1=minus_half[:], op=ALU.pow
            )

        def norm_on_gpsimd(m):
            if not VECTOR_PAIRS <= m < PAIRS:
                return
            start_norm(m)
            pair = slice(2 * m, 2 * m + 2)
            scaled = work.tile([P, 2, D], F32, tag="scaled")
            for a in range(2):
                n = 2 * m + a
                nc.gpsimd.tensor_scalar(
                    out=scaled[:, a, :].rearrange("p (u q e) -> p u q e", u=2, e=2),
                    in0=sorted_view(x2_all[:, n, :]),
                    scalar1=rstd[:, n : n + 1],
                    scalar2=0.0,
                    op0=ALU.mult,
                    op1=ALU.add,
                )
            nc.gpsimd.tensor_tensor(
                out=xn2_all[:, pair, :],
                in0=scaled[:],
                in1=gain_sorted[:].unsqueeze(1).to_broadcast([P, 2, D]),
                op=ALU.mult,
            )

        def norm_on_vector(m):
            if not 0 <= m < VECTOR_PAIRS:
                return
            for n in range(2 * m, 2 * m + 2):
                for u in range(2):
                    half = slice(u * (D // 2), (u + 1) * (D // 2))
                    nc.vector.scalar_tensor_tensor(
                        out=xn2_all[:, n, half].rearrange("p (q e) -> p q e", e=2),
                        in0=sorted_view(x2_all[:, n, :])[:, u, :, :],
                        scalar=rstd[:, n : n + 1],
                        in1=gain_sorted[:, half].rearrange("p (q e) -> p q e", e=2),
                        op0=ALU.mult,
                        op1=ALU.mult,
                    )

        def up_pass(u_columns, c, first):
            n = c // TILE_CHUNKS
            width = u_columns.shape[1]
            nc.tensor.matmul_mx(
                out=u_columns,
                lhsT=xn_codes[:, n, :].bitcast(FP8X4),
                lhsT_scale=xn_planes[:, n, :],
                rhs=up_codes[:, first : first + width].bitcast(FP8X4),
                rhs_scale=up_plane[:, first : first + width],
                start=True,
                stop=True,
            )

        def pieces(c):
            count = END_PIECES if c >= CHUNKS - END_CHUNKS else 1
            width = BANK // count
            return [slice(i * width, (i + 1) * width) for i in range(count)]

        def gate_half(c):
            if not 0 <= c < CHUNKS:
                return
            gate_bank = banks.tile([P, BANK], F32, tag="scalar")
            gate = gates.tile([P, BANK], F32)
            for columns in pieces(c):
                up_pass(gate_bank[:, columns], c, (c % TILE_CHUNKS) * BANK + columns.start)
            for columns in pieces(c):
                nc.scalar.activation(out=gate[:, columns], in_=gate_bank[:, columns], func=ACT.Silu)
            held[("gate", c)] = gate

        def value_half(c):
            if not 0 <= c < CHUNKS:
                return
            value_bank = banks.tile([P, BANK], F32, tag="vector")
            for columns in pieces(c):
                up_pass(value_bank[:, columns], c, F + (c % TILE_CHUNKS) * BANK + columns.start)
            b = c % STORE_CHUNKS
            if b == 0:
                h_part = results.tile([P, STORE_CHUNKS, BANK], F32)
                held["h part"] = h_part
            h_part = held["h part"]
            n = c // TILE_CHUNKS
            at_end = c >= CHUNKS - STORE_CHUNKS
            for columns in pieces(c):
                nc.vector.tensor_tensor(
                    out=h_part[:, b, columns],
                    in0=value_bank[:, columns],
                    in1=held[("gate", c)][:, columns],
                    op=ALU.mult,
                )
                if at_end:
                    first = (c % TILE_CHUNKS) * BANK + columns.start
                    nc.sync.dma_start(
                        out=h_dram[:, n, first : first + columns.stop - columns.start],
                        in_=h_part[:, b, columns],
                    )
            if b == STORE_CHUNKS - 1 and not at_end:
                last = (c % TILE_CHUNKS + 1) * BANK
                nc.sync.dma_start(
                    out=h_dram[:, n, last - STORE_CHUNKS * BANK : last],
                    in_=h_part[:].rearrange("p b c -> p (b c)"),
                )

        def gated_up(m, quarter):
            first = PAIR_CHUNKS * m + 2 * quarter
            for c in range(first, first + 2):
                gate_half(c + SKEW)
                value_half(c)

        with tc.manual_schedule():
            keep_warm(WARM_FIRST)
            flip("o", o_all, 0)
            group("o", 0)
            flip("o", o_all, 1)
            group("o", 1)
            quantise("o", o_codes, o_planes, 0)
            keep_warm(WARM_STEP)
            for s in range(PAIRS + LEAD):
                m = s - LEAD
                project(2 * s)
                if m < 0:
                    project(2 * s + 1)
                flip("xn", xn2_all, m + 1, is_sorted=True)
                flip("o", o_all, 2 * s + 2)
                flip("o", o_all, 2 * s + 3)
                add_residual(2 * s)
                if s == 0:
                    add_residual(2 * s + 1)
                    mean_square(2 * s)
                    mean_square(2 * s + 1)
                group("xn", m + 1)
                group("o", 2 * s + 2)
                group("o", 2 * s + 3)
                norm_on_vector(s - 2)
                gated_up(m, 0)
                quantise("o", o_codes, o_planes, s + 1)
                quantise("xn", xn_codes, xn_planes, m + 1)
                if s == 0:
                    broadcast_gain()
                if s - 1 < VECTOR_PAIRS:
                    start_norm(s - 1)
                norm_on_gpsimd(m + 3)
                gated_up(m, 1)
                if s > 0:
                    mean_square(2 * s)
                if m >= 0:
                    project(2 * s + 1)
                if s > 0:
                    add_residual(2 * s + 1)
                if -2 <= m < 0:
                    keep_warm(WARM_STEP)
                gated_up(m, 2)
                if 0 < s < LEAD:
                    mean_square(2 * s + 1)
                gated_up(m, 3)
                if m >= 0:
                    mean_square(2 * s + 1)
